import numpy as np
import ml_dtypes


def mxq(x, axis, fmt="e4m3"):
    dtype, down = {"e4m3": (ml_dtypes.float8_e4m3fn, 7), "e5m2": (ml_dtypes.float8_e5m2, 14)}[fmt]
    v = np.moveaxis(np.asarray(x, np.float32).astype(ml_dtypes.bfloat16).astype(np.float64), axis, -1)
    blocks = v.reshape(v.shape[:-1] + (-1, 32))
    amax = np.abs(blocks).max(-1, keepdims=True)
    byte = np.maximum(np.where(amax > 0, np.frexp(amax)[1] - 1 + 127, 0) - down, 1)
    scale = np.exp2(byte - 127.0)
    codes = (blocks / scale).astype(np.float32).astype(dtype).astype(np.float64)
    return np.moveaxis((codes * scale).reshape(v.shape), -1, axis)


WIDE = False


def mx_kscale(k):
    if not WIDE:
        return np.ones(k)
    levels = np.array([10, -10, 5, -5, 0])
    a = np.random.permutation(np.resize(levels, k // 512 * 4)).reshape(k // 512, 4)
    idx = np.arange(k)
    return np.exp2(a[idx // 512, idx % 128 // 32])


BF16 = ml_dtypes.bfloat16


def bf(x):
    return np.asarray(x, np.float32).astype(BF16)


def f64(x):
    return np.asarray(x).astype(np.float64)


E2M1 = np.array([0.0, 0.5, 1.0, 1.5, 2.0, 3.0, 4.0, 6.0, -0.0, -0.5, -1.0, -1.5, -2.0, -3.0, -4.0, -6.0])


def pack_weight(w, fmt):
    k, n = w.shape
    w = f64(bf(w)).reshape(k // 32, 32, n)
    amax = np.abs(w).max(1)
    if fmt == "e4m3":
        byte = np.frexp(amax)[1] - 1 + 127 - 7
    else:
        mant, ex = np.frexp(amax / 6.0)
        byte = np.where(mant > 0.5, ex, ex - 1) + 127
    byte = np.clip(np.where(amax > 0, byte, 1), 1, 254)
    scaled = (w * np.exp2(127.0 - byte)[:, None, :]).reshape(k, n).astype(np.float32)
    by_word = np.ascontiguousarray(scaled.reshape(k // 512, 128, 4, n).transpose(0, 1, 3, 2))
    if fmt == "e4m3":
        words = by_word.astype(ml_dtypes.float8_e4m3fn).view(np.uint8)
    else:
        c = by_word.astype(ml_dtypes.float4_e2m1fn).view(np.uint8) & 0xF
        words = c[..., 0::2] | (c[..., 1::2] << 4)
    return np.ascontiguousarray(words), np.ascontiguousarray(byte.astype(np.uint8).reshape(k // 512, 16, n))


def unpack_weight(words, scales, fmt):
    g, p, n, _ = words.shape
    if fmt == "e4m3":
        vals = np.ascontiguousarray(words).view(ml_dtypes.float8_e4m3fn).astype(np.float64)
    else:
        nib = np.empty((g, p, n, 4), np.uint8)
        nib[..., 0::2] = words & 0xF
        nib[..., 1::2] = words >> 4
        vals = E2M1[nib]
    vals = vals * np.repeat(np.exp2(scales.astype(np.float64) - 127.0), 8, axis=1)[..., None]
    return vals.transpose(0, 1, 3, 2).reshape(g * 512, n)


B, H = 1024, 1024
EPS = 1e-5
NUM_GROUPS = 4
FMT = "e4m3"


def sigmoid(v):
    return 1.0 / (1.0 + np.exp(-v))


def _group_norm(z, weight, bias):
    n, ch = z.shape
    zg = z.reshape(n, NUM_GROUPS, ch // NUM_GROUPS)
    mean = zg.mean(axis=-1, keepdims=True)
    var = zg.var(axis=-1, keepdims=True)
    zn = (zg - mean) / np.sqrt(var + EPS)
    return zn.reshape(n, ch) * weight + bias


def setup_inputs():
    s = mx_kscale(H)
    x = bf(np.random.standard_normal((1, B, H)))
    h = bf(np.random.standard_normal((B, H)) * s)
    c = bf(np.random.standard_normal((B, H)))
    w = np.random.uniform(-1.0, 1.0, (NUM_GROUPS * H, H)) / np.sqrt(H) / s[None, :]
    words, scales = pack_weight(np.ascontiguousarray(w.T), FMT)
    b = bf(np.random.standard_normal(NUM_GROUPS * H) * 0.3)
    gn_weight = bf(1.0 + 0.1 * np.random.standard_normal(NUM_GROUPS * H))
    gn_bias = bf(0.1 * np.random.standard_normal(NUM_GROUPS * H))
    return {"x": x,
            "h": h,
            "c": c,
            "W_words": words,
            "W_scales": scales,
            "b": b,
            "gn_weight": gn_weight,
            "gn_bias": gn_bias}


def reference(x, h, c, W_words, W_scales, b, gn_weight, gn_bias):
    lin = (mxq(f64(h), 1, "e4m3") @ unpack_weight(W_words, W_scales, FMT)) + f64(b)
    z = _group_norm(lin, f64(gn_weight), f64(gn_bias))
    i, f, o, g = np.split(z, NUM_GROUPS, axis=1)
    c_new = sigmoid(f) * f64(c) + sigmoid(i) * np.tanh(g)
    h_new = sigmoid(o) * np.tanh(c_new)
    return (h_new, c_new)

@@ -1,0 +1,207 @@
+from contextlib import ExitStack
+
+import concourse.mybir as mybir
+from concourse.masks import make_identity
+
+F32 = mybir.dt.float32
+BF16 = mybir.dt.bfloat16
+I32 = mybir.dt.int32
+U32 = mybir.dt.uint32
+U8 = mybir.dt.uint8
+FP8X4 = mybir.dt.float8_e4m3fn_x4
+ALU = mybir.AluOpType
+ACT = mybir.ActivationFunctionType
+
+P = 128
+PACK = 4
+K_PASS = P * PACK
+BATCH = 1024
+HIDDEN = 1024
+GATES = 4
+PASSES = HIDDEN // K_PASS
+ROW_TILES = BATCH // P
+BANK = 512
+BANKS_PER_GATE = HIDDEN // BANK
+EPS = 1e-5
+
+FLOPS = 2 * BATCH * HIDDEN * GATES * HIDDEN
+BYTES = (
+    2 * BATCH * HIDDEN * 2
+    + HIDDEN * GATES * HIDDEN
+    + HIDDEN // 32 * GATES * HIDDEN
+    + 3 * GATES * HIDDEN * 2
+    + 2 * BATCH * HIDDEN * 4
+)
+
+
+def tile_lstmcell2_kernel(
+    tc, x, h, c, W_words, W_scales, b, gn_weight, gn_bias, out_0, out_1
+):
+    nc = tc.nc
+    channels = GATES * HIDDEN
+    gate_funcs = [ACT.Sigmoid, ACT.Sigmoid, ACT.Sigmoid, ACT.Tanh]
+
+    with ExitStack() as stack:
+        keep = stack.enter_context(tc.tile_pool(name="keep", bufs=1))
+        stage = stack.enter_context(tc.tile_pool(name="stage", bufs=2))
+        work = stack.enter_context(tc.tile_pool(name="work", bufs=2))
+        small = stack.enter_context(tc.tile_pool(name="small", bufs=4))
+        psum = stack.enter_context(tc.psum_pool(name="psum", bufs=8))
+
+        w_planes = keep.tile([P, channels], U8, align_bytes=64)
+        nc.vector.memset(w_planes[:].bitcast(I32), 0)
+        scale_words = W_scales.bitcast(I32)
+        for quad in range(4):
+            nc.sync.dma_start(
+                out=w_planes[32 * quad : 32 * quad + 4 * PASSES, :].bitcast(I32),
+                in_=scale_words[:, 4 * quad : 4 * quad + 4, :],
+            )
+
+        w_words = keep.tile([P, PASSES, channels], U32, align_bytes=64)
+        for gate in range(GATES):
+            for g in range(PASSES):
+                gate_bytes = slice(gate * HIDDEN * PACK, (gate + 1) * HIDDEN * PACK)
+                nc.sync.dma_start(
+                    out=w_words[:, g, gate * HIDDEN : (gate + 1) * HIDDEN].bitcast(I32),
+                    in_=W_words[g].rearrange("p n t -> p (n t)")[:, gate_bytes].bitcast(I32),
+                )
+
+        b_all = keep.tile([P, channels], BF16)
+        gw_all = keep.tile([P, channels], BF16)
+        gb_all = keep.tile([P, channels], BF16)
+
+        ident = keep.tile([P, P], F32)
+        make_identity(nc, ident[:])
+        minus_half = keep.tile([P, 1], F32)
+        nc.gpsimd.memset(minus_half[:], -0.5)
+
+        h_codes = keep.tile([P, ROW_TILES, PASSES * P], U32, align_bytes=64)
+        h_scales = keep.tile([P, ROW_TILES, PASSES * P], U8, align_bytes=64)
+
+        def quantise_h_row_tile(rt):
+            h_raw = stage.tile([P, HIDDEN], BF16, bufs=4)
+            nc.scalar.dma_start(out=h_raw[:], in_=h[rt * P : (rt + 1) * P, :])
+            h_pairs = h_raw[:].bitcast(F32)
+            flipped = psum.tile([P, BANK], F32, tag="bank")
+            pairs_per_pass = K_PASS // 2
+            for g in range(PASSES):
+                for u in range(2):
+                    block = 2 * g + u
+                    nc.tensor.transpose(
+                        flipped[:, block * P : (block + 1) * P],
+                        h_pairs[:, pairs_per_pass * g + u : pairs_per_pass * (g + 1) : 2],
+                        ident[:],
+                    )
+            grouped = stage.tile([P, PASSES * P * PACK], BF16, align_bytes=64)
+            nc.vector.tensor_copy(
+                out=grouped[:].bitcast(F32).rearrange("p (g r u) -> p g r u", g=PASSES, u=2),
+                in_=flipped[:].rearrange("p (g u r) -> p g r u", g=PASSES, u=2),
+            )
+            nc.vector.quantize_mx(
+                out=h_codes[:, rt, :].bitcast(FP8X4),
+                scales=h_scales[:, rt, :],
+                in_=grouped[:],
+            )
+
+        quantise_h_row_tile(0)
+        nc.scalar.dma_start(out=b_all[:], in_=b.partition_broadcast(P))
+        nc.scalar.dma_start(out=gw_all[:], in_=gn_weight.partition_broadcast(P))
+        nc.scalar.dma_start(out=gb_all[:], in_=gn_bias.partition_broadcast(P))
+        for rt in range(1, ROW_TILES):
+            quantise_h_row_tile(rt)
+
+        for rt in range(ROW_TILES):
+            rows = slice(rt * P, (rt + 1) * P)
+            c_rows = work.tile([P, HIDDEN], BF16)
+            nc.sync.dma_start(out=c_rows[:], in_=c[rows, :])
+
+            gate_values = []
+            for gate in range(GATES):
+                gate_cols = slice(gate * HIDDEN, (gate + 1) * HIDDEN)
+                lin = work.tile([P, HIDDEN], F32, bufs=3)
+                sums = small.tile([P, BANKS_PER_GATE], F32)
+                for half in range(BANKS_PER_GATE):
+                    cols = slice(gate * HIDDEN + half * BANK, gate * HIDDEN + (half + 1) * BANK)
+                    acc = psum.tile([P, BANK], F32, tag="bank")
+                    for g in range(PASSES):
+                        nc.tensor.matmul_mx(
+                            out=acc[:],
+                            lhsT=h_codes[:, rt, g * P : (g + 1) * P].bitcast(FP8X4),
+                            lhsT_scale=h_scales[:, rt, g * P : (g + 1) * P],
+                            rhs=w_words[:, g, cols].bitcast(FP8X4),
+                            rhs_scale=w_planes[4 * g : P, cols],
+                            start=(g == 0),
+                            stop=(g == PASSES - 1),
+                        )
+                    nc.vector.scalar_tensor_tensor(
+                        out=lin[:, half * BANK : (half + 1) * BANK],
+                        in0=acc[:],
+                        scalar=1.0,
+                        in1=b_all[:, cols],
+                        op0=ALU.mult,
+                        op1=ALU.add,
+                        accum_out=sums[:, half : half + 1],
+                    )
+                neg_mean = small.tile([P, 1], F32)
+                nc.vector.tensor_scalar(
+                    out=neg_mean[:],
+                    in0=sums[:, 0:1],
+                    scalar1=sums[:, 1:2],
+                    scalar2=-1.0 / HIDDEN,
+                    op0=ALU.add,
+                    op1=ALU.mult,
+                )
+                squares = work.tile([P, HIDDEN], BF16, bufs=1)
+                sum_squares = small.tile([P, 1], F32)
+                nc.scalar.activation(
+                    out=squares[:],
+                    in_=lin[:],
+                    func=ACT.Square,
+                    bias=neg_mean[:],
+                    scale=1.0,
+                    accum_out=sum_squares[:],
+                )
+                var_eps = small.tile([P, 1], F32)
+                nc.gpsimd.tensor_scalar(
+                    out=var_eps[:],
+                    in0=sum_squares[:],
+                    scalar1=1.0 / HIDDEN,
+                    scalar2=EPS,
+                    op0=ALU.mult,
+                    op1=ALU.add,
+                )
+                rstd = small.tile([P, 1], F32)
+                nc.gpsimd.tensor_tensor(
+                    out=rstd[:], in0=var_eps[:], in1=minus_half[:], op=ALU.pow
+                )
+                nc.vector.scalar_tensor_tensor(
+                    out=lin[:],
+                    in0=lin[:],
+                    scalar=neg_mean[:],
+                    in1=gw_all[:, gate_cols],
+                    op0=ALU.add,
+                    op1=ALU.mult,
+                )
+                nc.vector.scalar_tensor_tensor(
+                    out=lin[:],
+                    in0=lin[:],
+                    scalar=rstd[:],
+                    in1=gb_all[:, gate_cols],
+                    op0=ALU.mult,
+                    op1=ALU.add,
+                )
+                value = work.tile([P, HIDDEN], F32, name="gate%d" % gate)
+                nc.scalar.activation(out=value[:], in_=lin[:], func=gate_funcs[gate])
+                gate_values.append(value)
+
+            i_gate, f_gate, o_gate, g_gate = gate_values
+            c_new = work.tile([P, HIDDEN], F32)
+            nc.vector.tensor_mul(out=f_gate[:], in0=f_gate[:], in1=c_rows[:])
+            nc.vector.tensor_mul(out=i_gate[:], in0=i_gate[:], in1=g_gate[:])
+            nc.vector.tensor_add(out=c_new[:], in0=f_gate[:], in1=i_gate[:])
+            nc.sync.dma_start(out=out_1[rows, :], in_=c_new[:])
+            tanh_c = work.tile([P, HIDDEN], F32)
+            nc.scalar.activation(out=tanh_c[:], in_=c_new[:], func=ACT.Tanh)
+            h_new = work.tile([P, HIDDEN], F32)
+            nc.vector.tensor_mul(out=h_new[:], in0=o_gate[:], in1=tanh_c[:])
+            nc.sync.dma_start(out=out_0[rows, :], in_=h_new[:])

@@ -22,6 +22,9 @@ PASSES = HIDDEN // K_PASS
 ROW_TILES = BATCH // P
 BANK = 512
 BANKS_PER_GATE = HIDDEN // BANK
+SUPER = BANK // P
+SUPER_TILES = ROW_TILES // SUPER
+CH_TILES = HIDDEN // P
 EPS = 1e-5
 
 FLOPS = 2 * BATCH * HIDDEN * GATES * HIDDEN
@@ -44,6 +47,7 @@ def tile_lstmcell2_kernel(
     with ExitStack() as stack:
         keep = stack.enter_context(tc.tile_pool(name="keep", bufs=1))
         stage = stack.enter_context(tc.tile_pool(name="stage", bufs=2))
+        normed = stack.enter_context(tc.tile_pool(name="normed", bufs=SUPER))
         work = stack.enter_context(tc.tile_pool(name="work", bufs=2))
         small = stack.enter_context(tc.tile_pool(name="small", bufs=4))
         psum = stack.enter_context(tc.psum_pool(name="psum", bufs=8))
@@ -66,12 +70,10 @@ def tile_lstmcell2_kernel(
                     in_=W_words[g].rearrange("p n t -> p (n t)")[:, gate_bytes].bitcast(I32),
                 )
 
-        b_all = keep.tile([P, channels], BF16)
-        gw_all = keep.tile([P, channels], BF16)
-        gb_all = keep.tile([P, channels], BF16)
-
         ident = keep.tile([P, P], F32)
         make_identity(nc, ident[:])
+        ident_bf16 = keep.tile([P, P], BF16)
+        make_identity(nc, ident_bf16[:])
         minus_half = keep.tile([P, 1], F32)
         nc.gpsimd.memset(minus_half[:], -0.5)
 
@@ -82,20 +84,20 @@ def tile_lstmcell2_kernel(
             h_raw = stage.tile([P, HIDDEN], BF16, bufs=4)
             nc.scalar.dma_start(out=h_raw[:], in_=h[rt * P : (rt + 1) * P, :])
             h_pairs = h_raw[:].bitcast(F32)
-            flipped = psum.tile([P, BANK], F32, tag="bank")
+            h_T = psum.tile([P, BANK], F32, tag="bank")
             pairs_per_pass = K_PASS // 2
             for g in range(PASSES):
                 for u in range(2):
                     block = 2 * g + u
                     nc.tensor.transpose(
-                        flipped[:, block * P : (block + 1) * P],
+                        h_T[:, block * P : (block + 1) * P],
                         h_pairs[:, pairs_per_pass * g + u : pairs_per_pass * (g + 1) : 2],
                         ident[:],
                     )
             grouped = stage.tile([P, PASSES * P * PACK], BF16, align_bytes=64)
             nc.vector.tensor_copy(
                 out=grouped[:].bitcast(F32).rearrange("p (g r u) -> p g r u", g=PASSES, u=2),
-                in_=flipped[:].rearrange("p (g u r) -> p g r u", g=PASSES, u=2),
+                in_=h_T[:].rearrange("p (g u r) -> p g r u", g=PASSES, u=2),
             )
             nc.vector.quantize_mx(
                 out=h_codes[:, rt, :].bitcast(FP8X4),
@@ -103,105 +105,158 @@ def tile_lstmcell2_kernel(
                 in_=grouped[:],
             )
 
-        quantise_h_row_tile(0)
-        nc.scalar.dma_start(out=b_all[:], in_=b.partition_broadcast(P))
-        nc.scalar.dma_start(out=gw_all[:], in_=gn_weight.partition_broadcast(P))
-        nc.scalar.dma_start(out=gb_all[:], in_=gn_bias.partition_broadcast(P))
-        for rt in range(1, ROW_TILES):
+        for rt in range(SUPER):
             quantise_h_row_tile(rt)
 
-        for rt in range(ROW_TILES):
-            rows = slice(rt * P, (rt + 1) * P)
-            c_rows = work.tile([P, HIDDEN], BF16)
-            nc.sync.dma_start(out=c_rows[:], in_=c[rows, :])
+        b_all = keep.tile([P, channels], BF16)
+        for gate in range(GATES):
+            gate_cols = slice(gate * HIDDEN, (gate + 1) * HIDDEN)
+            nc.scalar.dma_start(
+                out=b_all[:, gate_cols], in_=b[gate_cols].partition_broadcast(P)
+            )
 
-            gate_values = []
-            for gate in range(GATES):
-                gate_cols = slice(gate * HIDDEN, (gate + 1) * HIDDEN)
-                lin = work.tile([P, HIDDEN], F32, bufs=3)
-                sums = small.tile([P, BANKS_PER_GATE], F32)
-                for half in range(BANKS_PER_GATE):
-                    cols = slice(gate * HIDDEN + half * BANK, gate * HIDDEN + (half + 1) * BANK)
-                    acc = psum.tile([P, BANK], F32, tag="bank")
-                    for g in range(PASSES):
-                        nc.tensor.matmul_mx(
-                            out=acc[:],
-                            lhsT=h_codes[:, rt, g * P : (g + 1) * P].bitcast(FP8X4),
-                            lhsT_scale=h_scales[:, rt, g * P : (g + 1) * P],
-                            rhs=w_words[:, g, cols].bitcast(FP8X4),
-                            rhs_scale=w_planes[4 * g : P, cols],
-                            start=(g == 0),
-                            stop=(g == PASSES - 1),
-                        )
-                    nc.vector.scalar_tensor_tensor(
-                        out=lin[:, half * BANK : (half + 1) * BANK],
-                        in0=acc[:],
-                        scalar=1.0,
-                        in1=b_all[:, cols],
-                        op0=ALU.mult,
-                        op1=ALU.add,
-                        accum_out=sums[:, half : half + 1],
+        n_pieces = channels // P
+        gn_rows = keep.tile([P, P], BF16)
+        nc.vector.memset(gn_rows[:], 0.0)
+        nc.scalar.dma_start(
+            out=gn_rows[0:n_pieces, :], in_=gn_weight.rearrange("(t n) -> t n", n=P)
+        )
+        nc.scalar.dma_start(
+            out=gn_rows[n_pieces : 2 * n_pieces, :], in_=gn_bias.rearrange("(t n) -> t n", n=P)
+        )
+        gn_T = psum.tile([P, P], BF16, tag="bank")
+        nc.tensor.transpose(gn_T[:], gn_rows[:], ident_bf16[:])
+        gn_cols = keep.tile([P, 2 * n_pieces], F32)
+        nc.vector.tensor_copy(out=gn_cols[:], in_=gn_T[:, 0 : 2 * n_pieces])
+
+        def normalise_gate(rt, gate, x_rows):
+            lin = x_rows[:, gate * HIDDEN : (gate + 1) * HIDDEN]
+            sums = small.tile([P, BANKS_PER_GATE], F32)
+            for half in range(BANKS_PER_GATE):
+                cols = slice(gate * HIDDEN + half * BANK, gate * HIDDEN + (half + 1) * BANK)
+                acc = psum.tile([P, BANK], F32, tag="bank")
+                for g in range(PASSES):
+                    nc.tensor.matmul_mx(
+                        out=acc[:],
+                        lhsT=h_codes[:, rt, g * P : (g + 1) * P].bitcast(FP8X4),
+                        lhsT_scale=h_scales[:, rt, g * P : (g + 1) * P],
+                        rhs=w_words[:, g, cols].bitcast(FP8X4),
+                        rhs_scale=w_planes[4 * g : P, cols],
+                        start=(g == 0),
+                        stop=(g == PASSES - 1),
                     )
-                neg_mean = small.tile([P, 1], F32)
-                nc.vector.tensor_scalar(
-                    out=neg_mean[:],
-                    in0=sums[:, 0:1],
-                    scalar1=sums[:, 1:2],
-                    scalar2=-1.0 / HIDDEN,
-                    op0=ALU.add,
-                    op1=ALU.mult,
-                )
-                squares = work.tile([P, HIDDEN], BF16, bufs=1)
-                sum_squares = small.tile([P, 1], F32)
-                nc.scalar.activation(
-                    out=squares[:],
-                    in_=lin[:],
-                    func=ACT.Square,
-                    bias=neg_mean[:],
-                    scale=1.0,
-                    accum_out=sum_squares[:],
-                )
-                var_eps = small.tile([P, 1], F32)
-                nc.gpsimd.tensor_scalar(
-                    out=var_eps[:],
-                    in0=sum_squares[:],
-                    scalar1=1.0 / HIDDEN,
-                    scalar2=EPS,
+                nc.vector.scalar_tensor_tensor(
+                    out=lin[:, half * BANK : (half + 1) * BANK],
+                    in0=acc[:],
+                    scalar=1.0,
+                    in1=b_all[:, cols],
                     op0=ALU.mult,
                     op1=ALU.add,
+                    accum_out=sums[:, half : half + 1],
                 )
-                rstd = small.tile([P, 1], F32)
-                nc.gpsimd.tensor_tensor(
-                    out=rstd[:], in0=var_eps[:], in1=minus_half[:], op=ALU.pow
-                )
-                nc.vector.scalar_tensor_tensor(
-                    out=lin[:],
-                    in0=lin[:],
-                    scalar=neg_mean[:],
-                    in1=gw_all[:, gate_cols],
-                    op0=ALU.add,
-                    op1=ALU.mult,
-                )
-                nc.vector.scalar_tensor_tensor(
-                    out=lin[:],
-                    in0=lin[:],
-                    scalar=rstd[:],
-                    in1=gb_all[:, gate_cols],
-                    op0=ALU.mult,
-                    op1=ALU.add,
-                )
-                value = work.tile([P, HIDDEN], F32, name="gate%d" % gate)
-                nc.scalar.activation(out=value[:], in_=lin[:], func=gate_funcs[gate])
-                gate_values.append(value)
+            neg_mean = small.tile([P, 1], F32)
+            nc.vector.tensor_scalar(
+                out=neg_mean[:],
+                in0=sums[:, 0:1],
+                scalar1=sums[:, 1:2],
+                scalar2=-1.0 / HIDDEN,
+                op0=ALU.add,
+                op1=ALU.mult,
+            )
+            squares = work.tile([P, HIDDEN], BF16, bufs=1)
+            sum_squares = small.tile([P, 1], F32)
+            nc.scalar.activation(
+                out=squares[:],
+                in_=lin,
+                func=ACT.Square,
+                bias=neg_mean[:],
+                scale=1.0,
+                accum_out=sum_squares[:],
+            )
+            var_eps = small.tile([P, 1], F32)
+            nc.gpsimd.tensor_scalar(
+                out=var_eps[:],
+                in0=sum_squares[:],
+                scalar1=1.0 / HIDDEN,
+                scalar2=EPS,
+                op0=ALU.mult,
+                op1=ALU.add,
+            )
+            rstd = small.tile([P, 1], F32)
+            nc.gpsimd.tensor_tensor(out=rstd[:], in0=var_eps[:], in1=minus_half[:], op=ALU.pow)
+            nc.vector.tensor_scalar(
+                out=lin,
+                in0=lin,
+                scalar1=neg_mean[:],
+                scalar2=rstd[:],
+                op0=ALU.add,
+                op1=ALU.mult,
+            )
 
-            i_gate, f_gate, o_gate, g_gate = gate_values
-            c_new = work.tile([P, HIDDEN], F32)
-            nc.vector.tensor_mul(out=f_gate[:], in0=f_gate[:], in1=c_rows[:])
-            nc.vector.tensor_mul(out=i_gate[:], in0=i_gate[:], in1=g_gate[:])
-            nc.vector.tensor_add(out=c_new[:], in0=f_gate[:], in1=i_gate[:])
-            nc.sync.dma_start(out=out_1[rows, :], in_=c_new[:])
-            tanh_c = work.tile([P, HIDDEN], F32)
-            nc.scalar.activation(out=tanh_c[:], in_=c_new[:], func=ACT.Tanh)
-            h_new = work.tile([P, HIDDEN], F32)
-            nc.vector.tensor_mul(out=h_new[:], in0=o_gate[:], in1=tanh_c[:])
-            nc.sync.dma_start(out=out_0[rows, :], in_=h_new[:])
+        def store_transposed(value_T, out, s, j):
+            back = psum.tile([P, BANK], F32, tag="bank")
+            for q in range(SUPER):
+                nc.tensor.transpose(
+                    back[:, q * P : (q + 1) * P], value_T[:, q * P : (q + 1) * P], ident[:]
+                )
+            out_rows = work.tile([P, SUPER, P], F32, bufs=4)
+            nc.vector.tensor_copy(out=out_rows[:].rearrange("p q n -> p (q n)"), in_=back[:])
+            nc.sync.dma_start(
+                out=out[s * BANK : (s + 1) * BANK, j * P : (j + 1) * P].rearrange(
+                    "(q p) n -> p q n", p=P
+                ),
+                in_=out_rows[:],
+            )
+
+        for s in range(SUPER_TILES):
+            c_rows = stage.tile([P, SUPER, HIDDEN], BF16)
+            nc.sync.dma_start(
+                out=c_rows[:],
+                in_=c[s * BANK : (s + 1) * BANK, :].rearrange("(q p) n -> p q n", p=P),
+            )
+            if s > 0:
+                for q in range(SUPER):
+                    quantise_h_row_tile(s * SUPER + q)
+
+            x_tiles = [normed.tile([P, channels], F32, name="x_rows", tag="x_rows") for q in range(SUPER)]
+            for gate in range(GATES):
+                for q in range(SUPER):
+                    normalise_gate(s * SUPER + q, gate, x_tiles[q])
+
+            for j in range(CH_TILES):
+                gate_T = []
+                for gate in range(GATES):
+                    first = gate * HIDDEN + j * P
+                    x_T = psum.tile([P, BANK], F32, tag="bank")
+                    for q in range(SUPER):
+                        nc.tensor.transpose(
+                            x_T[:, q * P : (q + 1) * P], x_tiles[q][:, first : first + P], ident[:]
+                        )
+                    piece = gate * CH_TILES + j
+                    value = work.tile([P, BANK], F32, name="gate%d" % gate)
+                    nc.scalar.activation(
+                        out=value[:],
+                        in_=x_T[:],
+                        func=gate_funcs[gate],
+                        scale=gn_cols[:, piece : piece + 1],
+                        bias=gn_cols[:, n_pieces + piece : n_pieces + piece + 1],
+                    )
+                    gate_T.append(value)
+                i_T, f_T, o_T, g_T = gate_T
+
+                c_T = psum.tile([P, BANK], BF16, tag="bank")
+                for q in range(SUPER):
+                    nc.tensor.transpose(
+                        c_T[:, q * P : (q + 1) * P], c_rows[:, q, j * P : (j + 1) * P], ident_bf16[:]
+                    )
+
+                nc.vector.tensor_mul(out=f_T[:], in0=f_T[:], in1=c_T[:])
+                nc.vector.tensor_mul(out=i_T[:], in0=i_T[:], in1=g_T[:])
+                c_new_T = work.tile([P, BANK], F32)
+                nc.vector.tensor_add(out=c_new_T[:], in0=f_T[:], in1=i_T[:])
+                tanh_c_T = work.tile([P, BANK], F32)
+                nc.scalar.activation(out=tanh_c_T[:], in_=c_new_T[:], func=ACT.Tanh)
+                store_transposed(c_new_T, out_1, s, j)
+                h_new_T = work.tile([P, BANK], F32)
+                nc.vector.tensor_mul(out=h_new_T[:], in0=o_T[:], in1=tanh_c_T[:])
+                store_transposed(h_new_T, out_0, s, j)

@@ -26,6 +26,7 @@ SUPER = BANK // P
 SUPER_TILES = ROW_TILES // SUPER
 CH_TILES = HIDDEN // P
 EPS = 1e-5
+NORM_LAG = 2
 
 FLOPS = 2 * BATCH * HIDDEN * GATES * HIDDEN
 BYTES = (
@@ -42,15 +43,23 @@ def tile_lstmcell2_kernel(
 ):
     nc = tc.nc
     channels = GATES * HIDDEN
+    n_pieces = channels // P
     gate_funcs = [ACT.Sigmoid, ACT.Sigmoid, ACT.Sigmoid, ACT.Tanh]
 
     with ExitStack() as stack:
+        stack.enter_context(tc.manual_schedule())
         keep = stack.enter_context(tc.tile_pool(name="keep", bufs=1))
         stage = stack.enter_context(tc.tile_pool(name="stage", bufs=2))
         normed = stack.enter_context(tc.tile_pool(name="normed", bufs=SUPER))
-        work = stack.enter_context(tc.tile_pool(name="work", bufs=2))
-        small = stack.enter_context(tc.tile_pool(name="small", bufs=4))
+        work = stack.enter_context(tc.tile_pool(name="work", bufs=3))
+        small = stack.enter_context(tc.tile_pool(name="small", bufs=6))
         psum = stack.enter_context(tc.psum_pool(name="psum", bufs=8))
+
+        h_raw = []
+        for rt in range(ROW_TILES):
+            h_raw.append(stage.tile([P, HIDDEN], BF16, name="h_raw", tag="h_raw", bufs=ROW_TILES))
+        for rt in range(SUPER):
+            nc.scalar.dma_start(out=h_raw[rt][:], in_=h[rt * P : (rt + 1) * P, :])
 
         w_planes = keep.tile([P, channels], U8, align_bytes=64)
         nc.vector.memset(w_planes[:].bitcast(I32), 0)
@@ -62,13 +71,33 @@ def tile_lstmcell2_kernel(
             )
 
         w_words = keep.tile([P, PASSES, channels], U32, align_bytes=64)
+        b_all = keep.tile([P, channels], BF16)
+        gn_rows = keep.tile([P, P], BF16)
+        nc.vector.memset(gn_rows[:], 0.0)
         for gate in range(GATES):
+            gate_cols = slice(gate * HIDDEN, (gate + 1) * HIDDEN)
+            gate_bytes = slice(gate * HIDDEN * PACK, (gate + 1) * HIDDEN * PACK)
             for g in range(PASSES):
-                gate_bytes = slice(gate * HIDDEN * PACK, (gate + 1) * HIDDEN * PACK)
                 nc.sync.dma_start(
-                    out=w_words[:, g, gate * HIDDEN : (gate + 1) * HIDDEN].bitcast(I32),
+                    out=w_words[:, g, gate_cols].bitcast(I32),
                     in_=W_words[g].rearrange("p n t -> p (n t)")[:, gate_bytes].bitcast(I32),
                 )
+            nc.sync.dma_start(out=b_all[:, gate_cols], in_=b[gate_cols].partition_broadcast(P))
+        nc.sync.dma_start(
+            out=gn_rows[0:n_pieces, :], in_=gn_weight.rearrange("(t n) -> t n", n=P)
+        )
+        nc.sync.dma_start(
+            out=gn_rows[n_pieces : 2 * n_pieces, :], in_=gn_bias.rearrange("(t n) -> t n", n=P)
+        )
+        c_rows = []
+        for s in range(SUPER_TILES):
+            c_rows.append(stage.tile([P, SUPER, HIDDEN], BF16, name="c_rows", tag="c_rows"))
+        nc.sync.dma_start(out=c_rows[0][:], in_=c[0:BANK, :].rearrange("(q p) n -> p q n", p=P))
+        for rt in range(SUPER, ROW_TILES):
+            nc.sync.dma_start(out=h_raw[rt][:], in_=h[rt * P : (rt + 1) * P, :])
+        nc.sync.dma_start(
+            out=c_rows[1][:], in_=c[BANK : 2 * BANK, :].rearrange("(q p) n -> p q n", p=P)
+        )
 
         ident = keep.tile([P, P], F32)
         make_identity(nc, ident[:])
@@ -79,11 +108,10 @@ def tile_lstmcell2_kernel(
 
         h_codes = keep.tile([P, ROW_TILES, PASSES * P], U32, align_bytes=64)
         h_scales = keep.tile([P, ROW_TILES, PASSES * P], U8, align_bytes=64)
+        grouped = {}
 
-        def quantise_h_row_tile(rt):
-            h_raw = stage.tile([P, HIDDEN], BF16, bufs=4)
-            nc.scalar.dma_start(out=h_raw[:], in_=h[rt * P : (rt + 1) * P, :])
-            h_pairs = h_raw[:].bitcast(F32)
+        def group_h_row_tile(rt):
+            h_pairs = h_raw[rt][:].bitcast(F32)
             h_T = psum.tile([P, BANK], F32, tag="bank")
             pairs_per_pass = K_PASS // 2
             for g in range(PASSES):
@@ -94,43 +122,33 @@ def tile_lstmcell2_kernel(
                         h_pairs[:, pairs_per_pass * g + u : pairs_per_pass * (g + 1) : 2],
                         ident[:],
                     )
-            grouped = stage.tile([P, PASSES * P * PACK], BF16, align_bytes=64)
+            grouped[rt] = stage.tile(
+                [P, PASSES * P * PACK], BF16, name="grouped", tag="grouped", align_bytes=64
+            )
             nc.vector.tensor_copy(
-                out=grouped[:].bitcast(F32).rearrange("p (g r u) -> p g r u", g=PASSES, u=2),
+                out=grouped[rt][:].bitcast(F32).rearrange("p (g r u) -> p g r u", g=PASSES, u=2),
                 in_=h_T[:].rearrange("p (g u r) -> p g r u", g=PASSES, u=2),
             )
+
+        def quantise_h_row_tile(rt):
             nc.vector.quantize_mx(
                 out=h_codes[:, rt, :].bitcast(FP8X4),
                 scales=h_scales[:, rt, :],
-                in_=grouped[:],
+                in_=grouped[rt][:],
             )
 
-        for rt in range(SUPER):
-            quantise_h_row_tile(rt)
+        def quantise_h(s):
+            for q in range(SUPER + 1):
+                if q < SUPER:
+                    group_h_row_tile(s * SUPER + q)
+                if q >= 1:
+                    quantise_h_row_tile(s * SUPER + q - 1)
 
-        b_all = keep.tile([P, channels], BF16)
-        for gate in range(GATES):
-            gate_cols = slice(gate * HIDDEN, (gate + 1) * HIDDEN)
-            nc.scalar.dma_start(
-                out=b_all[:, gate_cols], in_=b[gate_cols].partition_broadcast(P)
-            )
+        stats = {}
 
-        n_pieces = channels // P
-        gn_rows = keep.tile([P, P], BF16)
-        nc.vector.memset(gn_rows[:], 0.0)
-        nc.scalar.dma_start(
-            out=gn_rows[0:n_pieces, :], in_=gn_weight.rearrange("(t n) -> t n", n=P)
-        )
-        nc.scalar.dma_start(
-            out=gn_rows[n_pieces : 2 * n_pieces, :], in_=gn_bias.rearrange("(t n) -> t n", n=P)
-        )
-        gn_T = psum.tile([P, P], BF16, tag="bank")
-        nc.tensor.transpose(gn_T[:], gn_rows[:], ident_bf16[:])
-        gn_cols = keep.tile([P, 2 * n_pieces], F32)
-        nc.vector.tensor_copy(out=gn_cols[:], in_=gn_T[:, 0 : 2 * n_pieces])
-
-        def normalise_gate(rt, gate, x_rows):
-            lin = x_rows[:, gate * HIDDEN : (gate + 1) * HIDDEN]
+        def sum_rows(s, unit, x_tiles):
+            gate, q = divmod(unit, SUPER)
+            rt = s * SUPER + q
             sums = small.tile([P, BANKS_PER_GATE], F32)
             for half in range(BANKS_PER_GATE):
                 cols = slice(gate * HIDDEN + half * BANK, gate * HIDDEN + (half + 1) * BANK)
@@ -146,7 +164,7 @@ def tile_lstmcell2_kernel(
                         stop=(g == PASSES - 1),
                     )
                 nc.vector.scalar_tensor_tensor(
-                    out=lin[:, half * BANK : (half + 1) * BANK],
+                    out=x_tiles[q][:, cols],
                     in0=acc[:],
                     scalar=1.0,
                     in1=b_all[:, cols],
@@ -167,7 +185,7 @@ def tile_lstmcell2_kernel(
             sum_squares = small.tile([P, 1], F32)
             nc.scalar.activation(
                 out=squares[:],
-                in_=lin,
+                in_=x_tiles[q][:, gate * HIDDEN : (gate + 1) * HIDDEN],
                 func=ACT.Square,
                 bias=neg_mean[:],
                 scale=1.0,
@@ -184,6 +202,12 @@ def tile_lstmcell2_kernel(
             )
             rstd = small.tile([P, 1], F32)
             nc.gpsimd.tensor_tensor(out=rstd[:], in0=var_eps[:], in1=minus_half[:], op=ALU.pow)
+            stats[unit] = (neg_mean, rstd)
+
+        def normalise(unit, x_tiles):
+            gate, q = divmod(unit, SUPER)
+            neg_mean, rstd = stats[unit]
+            lin = x_tiles[q][:, gate * HIDDEN : (gate + 1) * HIDDEN]
             nc.vector.tensor_scalar(
                 out=lin,
                 in0=lin,
@@ -193,7 +217,61 @@ def tile_lstmcell2_kernel(
                 op1=ALU.mult,
             )
 
-        def store_transposed(value_T, out, s, j):
+        gn_cols = keep.tile([P, 2 * n_pieces], F32)
+
+        def flip_gn_vectors():
+            gn_T = psum.tile([P, P], BF16, tag="bank")
+            nc.tensor.transpose(gn_T[:], gn_rows[:], ident_bf16[:])
+            nc.vector.tensor_copy(out=gn_cols[:], in_=gn_T[:, 0 : 2 * n_pieces])
+
+        flipped = {}
+
+        def gates(s, j, x_tiles):
+            for gate in range(GATES):
+                first = gate * HIDDEN + j * P
+                x_T = psum.tile([P, BANK], F32, tag="bank")
+                for q in range(SUPER):
+                    nc.tensor.transpose(
+                        x_T[:, q * P : (q + 1) * P], x_tiles[q][:, first : first + P], ident[:]
+                    )
+                piece = gate * CH_TILES + j
+                value = work.tile([P, BANK], F32, name="gate%d" % gate)
+                nc.scalar.activation(
+                    out=value[:],
+                    in_=x_T[:],
+                    func=gate_funcs[gate],
+                    scale=gn_cols[:, piece : piece + 1],
+                    bias=gn_cols[:, n_pieces + piece : n_pieces + piece + 1],
+                )
+                flipped[("gate", gate, j)] = value
+            c_T = psum.tile([P, BANK], BF16, tag="bank")
+            for q in range(SUPER):
+                nc.tensor.transpose(
+                    c_T[:, q * P : (q + 1) * P], c_rows[s][:, q, j * P : (j + 1) * P], ident_bf16[:]
+                )
+            flipped[("c", j)] = c_T
+
+        def cell(j):
+            i_T = flipped[("gate", 0, j)]
+            f_T = flipped[("gate", 1, j)]
+            g_T = flipped[("gate", 3, j)]
+            nc.vector.tensor_mul(out=f_T[:], in0=f_T[:], in1=flipped[("c", j)][:])
+            nc.vector.tensor_mul(out=i_T[:], in0=i_T[:], in1=g_T[:])
+            c_new_T = work.tile([P, BANK], F32)
+            nc.vector.tensor_add(out=c_new_T[:], in0=f_T[:], in1=i_T[:])
+            tanh_c_T = work.tile([P, BANK], F32)
+            nc.scalar.activation(out=tanh_c_T[:], in_=c_new_T[:], func=ACT.Tanh)
+            flipped[("c_new", j)] = c_new_T
+            flipped[("tanh_c", j)] = tanh_c_T
+
+        def hidden(j):
+            h_new_T = work.tile([P, BANK], F32)
+            nc.vector.tensor_mul(
+                out=h_new_T[:], in0=flipped[("gate", 2, j)][:], in1=flipped[("tanh_c", j)][:]
+            )
+            flipped[("h_new", j)] = h_new_T
+
+        def store_as_rows(value_T, out, s, j):
             back = psum.tile([P, BANK], F32, tag="bank")
             for q in range(SUPER):
                 nc.tensor.transpose(
@@ -208,55 +286,31 @@ def tile_lstmcell2_kernel(
                 in_=out_rows[:],
             )
 
+        quantise_h(0)
+        units = GATES * SUPER
         for s in range(SUPER_TILES):
-            c_rows = stage.tile([P, SUPER, HIDDEN], BF16)
-            nc.sync.dma_start(
-                out=c_rows[:],
-                in_=c[s * BANK : (s + 1) * BANK, :].rearrange("(q p) n -> p q n", p=P),
-            )
-            if s > 0:
-                for q in range(SUPER):
-                    quantise_h_row_tile(s * SUPER + q)
+            x_tiles = []
+            for q in range(SUPER):
+                x_tiles.append(normed.tile([P, channels], F32, name="x_rows", tag="x_rows"))
 
-            x_tiles = [normed.tile([P, channels], F32, name="x_rows", tag="x_rows") for q in range(SUPER)]
-            for gate in range(GATES):
-                for q in range(SUPER):
-                    normalise_gate(s * SUPER + q, gate, x_tiles[q])
+            for unit in range(units + NORM_LAG):
+                if unit < units:
+                    sum_rows(s, unit, x_tiles)
+                if unit >= NORM_LAG:
+                    normalise(unit - NORM_LAG, x_tiles)
 
-            for j in range(CH_TILES):
-                gate_T = []
-                for gate in range(GATES):
-                    first = gate * HIDDEN + j * P
-                    x_T = psum.tile([P, BANK], F32, tag="bank")
-                    for q in range(SUPER):
-                        nc.tensor.transpose(
-                            x_T[:, q * P : (q + 1) * P], x_tiles[q][:, first : first + P], ident[:]
-                        )
-                    piece = gate * CH_TILES + j
-                    value = work.tile([P, BANK], F32, name="gate%d" % gate)
-                    nc.scalar.activation(
-                        out=value[:],
-                        in_=x_T[:],
-                        func=gate_funcs[gate],
-                        scale=gn_cols[:, piece : piece + 1],
-                        bias=gn_cols[:, n_pieces + piece : n_pieces + piece + 1],
-                    )
-                    gate_T.append(value)
-                i_T, f_T, o_T, g_T = gate_T
+            if s == 0:
+                flip_gn_vectors()
+            if s + 1 < SUPER_TILES:
+                quantise_h(s + 1)
 
-                c_T = psum.tile([P, BANK], BF16, tag="bank")
-                for q in range(SUPER):
-                    nc.tensor.transpose(
-                        c_T[:, q * P : (q + 1) * P], c_rows[:, q, j * P : (j + 1) * P], ident_bf16[:]
-                    )
-
-                nc.vector.tensor_mul(out=f_T[:], in0=f_T[:], in1=c_T[:])
-                nc.vector.tensor_mul(out=i_T[:], in0=i_T[:], in1=g_T[:])
-                c_new_T = work.tile([P, BANK], F32)
-                nc.vector.tensor_add(out=c_new_T[:], in0=f_T[:], in1=i_T[:])
-                tanh_c_T = work.tile([P, BANK], F32)
-                nc.scalar.activation(out=tanh_c_T[:], in_=c_new_T[:], func=ACT.Tanh)
-                store_transposed(c_new_T, out_1, s, j)
-                h_new_T = work.tile([P, BANK], F32)
-                nc.vector.tensor_mul(out=h_new_T[:], in0=o_T[:], in1=tanh_c_T[:])
-                store_transposed(h_new_T, out_0, s, j)
+            for j in range(CH_TILES + 2):
+                if j >= 2:
+                    hidden(j - 2)
+                if j < CH_TILES:
+                    gates(s, j, x_tiles)
+                if 1 <= j <= CH_TILES:
+                    cell(j - 1)
+                if j >= 2:
+                    store_as_rows(flipped[("c_new", j - 2)], out_1, s, j - 2)
+                    store_as_rows(flipped[("h_new", j - 2)], out_0, s, j - 2)

@@ -26,7 +26,8 @@ SUPER = BANK // P
 SUPER_TILES = ROW_TILES // SUPER
 CH_TILES = HIDDEN // P
 EPS = 1e-5
-NORM_LAG = 2
+STD_LAG = 2
+NORM_LAG = 3
 
 FLOPS = 2 * BATCH * HIDDEN * GATES * HIDDEN
 BYTES = (
@@ -52,7 +53,7 @@ def tile_lstmcell2_kernel(
         stage = stack.enter_context(tc.tile_pool(name="stage", bufs=2))
         normed = stack.enter_context(tc.tile_pool(name="normed", bufs=SUPER))
         work = stack.enter_context(tc.tile_pool(name="work", bufs=3))
-        small = stack.enter_context(tc.tile_pool(name="small", bufs=6))
+        small = stack.enter_context(tc.tile_pool(name="small", bufs=8))
         psum = stack.enter_context(tc.psum_pool(name="psum", bufs=8))
 
         h_raw = []
@@ -191,10 +192,14 @@ def tile_lstmcell2_kernel(
                 scale=1.0,
                 accum_out=sum_squares[:],
             )
+            stats[("neg_mean", unit)] = neg_mean
+            stats[("sum_squares", unit)] = sum_squares
+
+        def inverse_std(unit):
             var_eps = small.tile([P, 1], F32)
-            nc.gpsimd.tensor_scalar(
+            nc.vector.tensor_scalar(
                 out=var_eps[:],
-                in0=sum_squares[:],
+                in0=stats[("sum_squares", unit)][:],
                 scalar1=1.0 / HIDDEN,
                 scalar2=EPS,
                 op0=ALU.mult,
@@ -202,13 +207,15 @@ def tile_lstmcell2_kernel(
             )
             rstd = small.tile([P, 1], F32)
             nc.gpsimd.tensor_tensor(out=rstd[:], in0=var_eps[:], in1=minus_half[:], op=ALU.pow)
-            stats[unit] = (neg_mean, rstd)
+            stats[("rstd", unit)] = rstd
 
         def normalise(unit, x_tiles):
             gate, q = divmod(unit, SUPER)
-            neg_mean, rstd = stats[unit]
+            neg_mean = stats[("neg_mean", unit)]
+            rstd = stats[("rstd", unit)]
             lin = x_tiles[q][:, gate * HIDDEN : (gate + 1) * HIDDEN]
-            nc.vector.tensor_scalar(
+            engine = nc.vector if q == SUPER - 1 else nc.gpsimd
+            engine.tensor_scalar(
                 out=lin,
                 in0=lin,
                 scalar1=neg_mean[:],
@@ -294,10 +301,12 @@ def tile_lstmcell2_kernel(
                 x_tiles.append(normed.tile([P, channels], F32, name="x_rows", tag="x_rows"))
 
             for unit in range(units + NORM_LAG):
-                if unit < units:
-                    sum_rows(s, unit, x_tiles)
                 if unit >= NORM_LAG:
                     normalise(unit - NORM_LAG, x_tiles)
+                if unit < units:
+                    sum_rows(s, unit, x_tiles)
+                if STD_LAG <= unit < units + STD_LAG:
+                    inverse_std(unit - STD_LAG)
 
             if s == 0:
                 flip_gn_vectors()

@@ -26,8 +26,7 @@ SUPER = BANK // P
 SUPER_TILES = ROW_TILES // SUPER
 CH_TILES = HIDDEN // P
 EPS = 1e-5
-STD_LAG = 2
-NORM_LAG = 3
+NORM_LAG = 2
 
 FLOPS = 2 * BATCH * HIDDEN * GATES * HIDDEN
 BYTES = (
@@ -53,7 +52,7 @@ def tile_lstmcell2_kernel(
         stage = stack.enter_context(tc.tile_pool(name="stage", bufs=2))
         normed = stack.enter_context(tc.tile_pool(name="normed", bufs=SUPER))
         work = stack.enter_context(tc.tile_pool(name="work", bufs=3))
-        small = stack.enter_context(tc.tile_pool(name="small", bufs=8))
+        small = stack.enter_context(tc.tile_pool(name="small", bufs=6))
         psum = stack.enter_context(tc.psum_pool(name="psum", bufs=8))
 
         h_raw = []
@@ -126,7 +125,7 @@ def tile_lstmcell2_kernel(
             grouped[rt] = stage.tile(
                 [P, PASSES * P * PACK], BF16, name="grouped", tag="grouped", align_bytes=64
             )
-            nc.vector.tensor_copy(
+            nc.scalar.copy(
                 out=grouped[rt][:].bitcast(F32).rearrange("p (g r u) -> p g r u", g=PASSES, u=2),
                 in_=h_T[:].rearrange("p (g u r) -> p g r u", g=PASSES, u=2),
             )
@@ -192,14 +191,10 @@ def tile_lstmcell2_kernel(
                 scale=1.0,
                 accum_out=sum_squares[:],
             )
-            stats[("neg_mean", unit)] = neg_mean
-            stats[("sum_squares", unit)] = sum_squares
-
-        def inverse_std(unit):
             var_eps = small.tile([P, 1], F32)
-            nc.vector.tensor_scalar(
+            nc.gpsimd.tensor_scalar(
                 out=var_eps[:],
-                in0=stats[("sum_squares", unit)][:],
+                in0=sum_squares[:],
                 scalar1=1.0 / HIDDEN,
                 scalar2=EPS,
                 op0=ALU.mult,
@@ -207,22 +202,27 @@ def tile_lstmcell2_kernel(
             )
             rstd = small.tile([P, 1], F32)
             nc.gpsimd.tensor_tensor(out=rstd[:], in0=var_eps[:], in1=minus_half[:], op=ALU.pow)
-            stats[("rstd", unit)] = rstd
+            shift = small.tile([P, 1], F32)
+            nc.gpsimd.tensor_tensor(out=shift[:], in0=neg_mean[:], in1=rstd[:], op=ALU.mult)
+            stats[unit] = (neg_mean, rstd, shift)
 
         def normalise(unit, x_tiles):
             gate, q = divmod(unit, SUPER)
-            neg_mean = stats[("neg_mean", unit)]
-            rstd = stats[("rstd", unit)]
+            neg_mean, rstd, shift = stats[unit]
             lin = x_tiles[q][:, gate * HIDDEN : (gate + 1) * HIDDEN]
-            engine = nc.vector if q == SUPER - 1 else nc.gpsimd
-            engine.tensor_scalar(
-                out=lin,
-                in0=lin,
-                scalar1=neg_mean[:],
-                scalar2=rstd[:],
-                op0=ALU.add,
-                op1=ALU.mult,
-            )
+            if q % 2 == 0:
+                nc.vector.tensor_scalar(
+                    out=lin,
+                    in0=lin,
+                    scalar1=neg_mean[:],
+                    scalar2=rstd[:],
+                    op0=ALU.add,
+                    op1=ALU.mult,
+                )
+            else:
+                nc.scalar.activation(
+                    out=lin, in_=lin, func=ACT.Identity, scale=rstd[:], bias=shift[:]
+                )
 
         gn_cols = keep.tile([P, 2 * n_pieces], F32)
 
@@ -266,32 +266,38 @@ def tile_lstmcell2_kernel(
             nc.vector.tensor_mul(out=i_T[:], in0=i_T[:], in1=g_T[:])
             c_new_T = work.tile([P, BANK], F32)
             nc.vector.tensor_add(out=c_new_T[:], in0=f_T[:], in1=i_T[:])
-            tanh_c_T = work.tile([P, BANK], F32)
-            nc.scalar.activation(out=tanh_c_T[:], in_=c_new_T[:], func=ACT.Tanh)
             flipped[("c_new", j)] = c_new_T
-            flipped[("tanh_c", j)] = tanh_c_T
 
-        def hidden(j):
-            h_new_T = work.tile([P, BANK], F32)
-            nc.vector.tensor_mul(
-                out=h_new_T[:], in0=flipped[("gate", 2, j)][:], in1=flipped[("tanh_c", j)][:]
-            )
-            flipped[("h_new", j)] = h_new_T
+        rows = {}
 
-        def store_as_rows(value_T, out, s, j):
+        def flip_back(name, value_T, j):
             back = psum.tile([P, BANK], F32, tag="bank")
             for q in range(SUPER):
                 nc.tensor.transpose(
                     back[:, q * P : (q + 1) * P], value_T[:, q * P : (q + 1) * P], ident[:]
                 )
-            out_rows = work.tile([P, SUPER, P], F32, bufs=4)
-            nc.vector.tensor_copy(out=out_rows[:].rearrange("p q n -> p (q n)"), in_=back[:])
+            rows[(name, j)] = back
+
+        def tanh_of_cell(j):
+            tanh_c = work.tile([P, BANK], F32)
+            nc.scalar.activation(out=tanh_c[:], in_=rows[("c_new", j)][:], func=ACT.Tanh)
+            rows[("tanh_c", j)] = tanh_c
+
+        def store_rows(value, out, s, j):
             nc.sync.dma_start(
                 out=out[s * BANK : (s + 1) * BANK, j * P : (j + 1) * P].rearrange(
                     "(q p) n -> p q n", p=P
                 ),
-                in_=out_rows[:],
+                in_=value[:].rearrange("p (q n) -> p q n", q=SUPER),
             )
+
+        def outputs(s, j):
+            c_new = work.tile([P, BANK], F32)
+            nc.vector.tensor_copy(out=c_new[:], in_=rows[("c_new", j)][:])
+            store_rows(c_new, out_1, s, j)
+            h_new = work.tile([P, BANK], F32)
+            nc.vector.tensor_mul(out=h_new[:], in0=rows[("o", j)][:], in1=rows[("tanh_c", j)][:])
+            store_rows(h_new, out_0, s, j)
 
         quantise_h(0)
         units = GATES * SUPER
@@ -301,12 +307,10 @@ def tile_lstmcell2_kernel(
                 x_tiles.append(normed.tile([P, channels], F32, name="x_rows", tag="x_rows"))
 
             for unit in range(units + NORM_LAG):
-                if unit >= NORM_LAG:
-                    normalise(unit - NORM_LAG, x_tiles)
                 if unit < units:
                     sum_rows(s, unit, x_tiles)
-                if STD_LAG <= unit < units + STD_LAG:
-                    inverse_std(unit - STD_LAG)
+                if unit >= NORM_LAG:
+                    normalise(unit - NORM_LAG, x_tiles)
 
             if s == 0:
                 flip_gn_vectors()
@@ -315,11 +319,12 @@ def tile_lstmcell2_kernel(
 
             for j in range(CH_TILES + 2):
                 if j >= 2:
-                    hidden(j - 2)
+                    tanh_of_cell(j - 2)
                 if j < CH_TILES:
                     gates(s, j, x_tiles)
                 if 1 <= j <= CH_TILES:
                     cell(j - 1)
+                    flip_back("c_new", flipped[("c_new", j - 1)], j - 1)
+                    flip_back("o", flipped[("gate", 2, j - 1)], j - 1)
                 if j >= 2:
-                    store_as_rows(flipped[("c_new", j - 2)], out_1, s, j - 2)
-                    store_as_rows(flipped[("h_new", j - 2)], out_0, s, j - 2)
+                    outputs(s, j - 2)

@@ -237,6 +237,11 @@ def tile_lstmcell2_kernel(
             for gate in range(GATES):
                 first = gate * HIDDEN + j * P
                 x_T = psum.tile([P, BANK], F32, tag="bank")
+                if gate % 2 == 0:
+                    nc.tensor.matmul(
+                        out=x_T[:], lhsT=ident_bf16[:], rhs=c_rows[s][:, 0, 0:BANK],
+                        start=True, stop=True,
+                    )
                 for q in range(SUPER):
                     nc.tensor.transpose(
                         x_T[:, q * P : (q + 1) * P], x_tiles[q][:, first : first + P], ident[:]

@@ -18,22 +18,29 @@ K_PASS = P * PACK
 BATCH = 1024
 HIDDEN = 1024
 GATES = 4
+GATE_I, GATE_F, GATE_O, GATE_G = 0, 1, 2, 3
+CHANNELS = GATES * HIDDEN
 PASSES = HIDDEN // K_PASS
 ROW_TILES = BATCH // P
 BANK = 512
 BANKS_PER_GATE = HIDDEN // BANK
-SUPER = BANK // P
-SUPER_TILES = ROW_TILES // SUPER
-CH_TILES = HIDDEN // P
 EPS = 1e-5
-NORM_LAG = 2
 
-FLOPS = 2 * BATCH * HIDDEN * GATES * HIDDEN
+UNITS = GATES * ROW_TILES
+H_LEAD = 2
+GROUP = 4
+NORM_LAG = 2 * GROUP
+
+SUPER = BANK // P
+CH_TILES = HIDDEN // P
+PIECES = (ROW_TILES // SUPER) * CH_TILES
+
+FLOPS = 2 * BATCH * HIDDEN * CHANNELS
 BYTES = (
     2 * BATCH * HIDDEN * 2
-    + HIDDEN * GATES * HIDDEN
-    + HIDDEN // 32 * GATES * HIDDEN
-    + 3 * GATES * HIDDEN * 2
+    + HIDDEN * CHANNELS
+    + HIDDEN // 32 * CHANNELS
+    + 3 * CHANNELS * 2
     + 2 * BATCH * HIDDEN * 4
 )
 
@@ -42,294 +49,308 @@ def tile_lstmcell2_kernel(
     tc, x, h, c, W_words, W_scales, b, gn_weight, gn_bias, out_0, out_1
 ):
     nc = tc.nc
-    channels = GATES * HIDDEN
-    n_pieces = channels // P
-    gate_funcs = [ACT.Sigmoid, ACT.Sigmoid, ACT.Sigmoid, ACT.Tanh]
+    gn_pieces = CHANNELS // P
 
-    with ExitStack() as stack:
-        stack.enter_context(tc.manual_schedule())
-        keep = stack.enter_context(tc.tile_pool(name="keep", bufs=1))
-        stage = stack.enter_context(tc.tile_pool(name="stage", bufs=2))
-        normed = stack.enter_context(tc.tile_pool(name="normed", bufs=SUPER))
-        work = stack.enter_context(tc.tile_pool(name="work", bufs=3))
-        small = stack.enter_context(tc.tile_pool(name="small", bufs=6))
-        psum = stack.enter_context(tc.psum_pool(name="psum", bufs=8))
-
-        h_raw = []
-        for rt in range(ROW_TILES):
-            h_raw.append(stage.tile([P, HIDDEN], BF16, name="h_raw", tag="h_raw", bufs=ROW_TILES))
-        for rt in range(SUPER):
-            nc.scalar.dma_start(out=h_raw[rt][:], in_=h[rt * P : (rt + 1) * P, :])
-
-        w_planes = keep.tile([P, channels], U8, align_bytes=64)
-        nc.vector.memset(w_planes[:].bitcast(I32), 0)
-        scale_words = W_scales.bitcast(I32)
-        for quad in range(4):
-            nc.sync.dma_start(
-                out=w_planes[32 * quad : 32 * quad + 4 * PASSES, :].bitcast(I32),
-                in_=scale_words[:, 4 * quad : 4 * quad + 4, :],
-            )
-
-        w_words = keep.tile([P, PASSES, channels], U32, align_bytes=64)
-        b_all = keep.tile([P, channels], BF16)
-        gn_rows = keep.tile([P, P], BF16)
-        nc.vector.memset(gn_rows[:], 0.0)
-        for gate in range(GATES):
-            gate_cols = slice(gate * HIDDEN, (gate + 1) * HIDDEN)
-            gate_bytes = slice(gate * HIDDEN * PACK, (gate + 1) * HIDDEN * PACK)
-            for g in range(PASSES):
-                nc.sync.dma_start(
-                    out=w_words[:, g, gate_cols].bitcast(I32),
-                    in_=W_words[g].rearrange("p n t -> p (n t)")[:, gate_bytes].bitcast(I32),
-                )
-            nc.sync.dma_start(out=b_all[:, gate_cols], in_=b[gate_cols].partition_broadcast(P))
-        nc.sync.dma_start(
-            out=gn_rows[0:n_pieces, :], in_=gn_weight.rearrange("(t n) -> t n", n=P)
-        )
-        nc.sync.dma_start(
-            out=gn_rows[n_pieces : 2 * n_pieces, :], in_=gn_bias.rearrange("(t n) -> t n", n=P)
-        )
-        c_rows = []
-        for s in range(SUPER_TILES):
-            c_rows.append(stage.tile([P, SUPER, HIDDEN], BF16, name="c_rows", tag="c_rows"))
-        nc.sync.dma_start(out=c_rows[0][:], in_=c[0:BANK, :].rearrange("(q p) n -> p q n", p=P))
-        for rt in range(SUPER, ROW_TILES):
-            nc.sync.dma_start(out=h_raw[rt][:], in_=h[rt * P : (rt + 1) * P, :])
-        nc.sync.dma_start(
-            out=c_rows[1][:], in_=c[BANK : 2 * BANK, :].rearrange("(q p) n -> p q n", p=P)
-        )
+    with ExitStack() as whole:
+        whole.enter_context(tc.manual_schedule())
+        keep = whole.enter_context(tc.tile_pool(name="keep", bufs=1))
+        small = whole.enter_context(tc.tile_pool(name="small", bufs=4))
+        psum = whole.enter_context(tc.psum_pool(name="psum", bufs=8))
 
         ident = keep.tile([P, P], F32)
         make_identity(nc, ident[:])
         ident_bf16 = keep.tile([P, P], BF16)
         make_identity(nc, ident_bf16[:])
-        minus_half = keep.tile([P, 1], F32)
+        minus_half = keep.tile([P, GROUP], F32)
         nc.gpsimd.memset(minus_half[:], -0.5)
 
-        h_codes = keep.tile([P, ROW_TILES, PASSES * P], U32, align_bytes=64)
-        h_scales = keep.tile([P, ROW_TILES, PASSES * P], U8, align_bytes=64)
-        grouped = {}
+        x_rows = keep.tile([P, ROW_TILES, CHANNELS], F32)
+        c_rows = keep.tile([P, ROW_TILES, HIDDEN], BF16)
+        gn_rows = keep.tile([P, P], BF16)
+        gn_cols = keep.tile([P, 2 * gn_pieces], F32)
 
-        def group_h_row_tile(rt):
-            h_pairs = h_raw[rt][:].bitcast(F32)
-            h_T = psum.tile([P, BANK], F32, tag="bank")
-            pairs_per_pass = K_PASS // 2
-            for g in range(PASSES):
-                for u in range(2):
-                    block = 2 * g + u
-                    nc.tensor.transpose(
-                        h_T[:, block * P : (block + 1) * P],
-                        h_pairs[:, pairs_per_pass * g + u : pairs_per_pass * (g + 1) : 2],
-                        ident[:],
-                    )
-            grouped[rt] = stage.tile(
-                [P, PASSES * P * PACK], BF16, name="grouped", tag="grouped", align_bytes=64
-            )
-            nc.scalar.copy(
-                out=grouped[rt][:].bitcast(F32).rearrange("p (g r u) -> p g r u", g=PASSES, u=2),
-                in_=h_T[:].rearrange("p (g u r) -> p g r u", g=PASSES, u=2),
-            )
+        with ExitStack() as phase:
+            weights = phase.enter_context(tc.tile_pool(name="weights", bufs=1))
+            stage = phase.enter_context(tc.tile_pool(name="stage", bufs=3))
 
-        def quantise_h_row_tile(rt):
-            nc.vector.quantize_mx(
-                out=h_codes[:, rt, :].bitcast(FP8X4),
-                scales=h_scales[:, rt, :],
-                in_=grouped[rt][:],
-            )
+            h_raw = weights.tile([P, ROW_TILES, HIDDEN], BF16)
+            for rt in range(SUPER):
+                nc.scalar.dma_start(out=h_raw[:, rt, :], in_=h[rt * P : (rt + 1) * P, :])
 
-        def quantise_h(s):
-            for q in range(SUPER + 1):
-                if q < SUPER:
-                    group_h_row_tile(s * SUPER + q)
-                if q >= 1:
-                    quantise_h_row_tile(s * SUPER + q - 1)
-
-        stats = {}
-
-        def sum_rows(s, unit, x_tiles):
-            gate, q = divmod(unit, SUPER)
-            rt = s * SUPER + q
-            sums = small.tile([P, BANKS_PER_GATE], F32)
-            for half in range(BANKS_PER_GATE):
-                cols = slice(gate * HIDDEN + half * BANK, gate * HIDDEN + (half + 1) * BANK)
-                acc = psum.tile([P, BANK], F32, tag="bank")
-                for g in range(PASSES):
-                    nc.tensor.matmul_mx(
-                        out=acc[:],
-                        lhsT=h_codes[:, rt, g * P : (g + 1) * P].bitcast(FP8X4),
-                        lhsT_scale=h_scales[:, rt, g * P : (g + 1) * P],
-                        rhs=w_words[:, g, cols].bitcast(FP8X4),
-                        rhs_scale=w_planes[4 * g : P, cols],
-                        start=(g == 0),
-                        stop=(g == PASSES - 1),
-                    )
-                nc.vector.scalar_tensor_tensor(
-                    out=x_tiles[q][:, cols],
-                    in0=acc[:],
-                    scalar=1.0,
-                    in1=b_all[:, cols],
-                    op0=ALU.mult,
-                    op1=ALU.add,
-                    accum_out=sums[:, half : half + 1],
+            w_planes = weights.tile([P, CHANNELS], U8, align_bytes=64)
+            nc.vector.memset(w_planes[:].bitcast(I32), 0)
+            scale_words = W_scales.bitcast(I32)
+            for quad in range(4):
+                nc.sync.dma_start(
+                    out=w_planes[32 * quad : 32 * quad + 4 * PASSES, :].bitcast(I32),
+                    in_=scale_words[:, 4 * quad : 4 * quad + 4, :],
                 )
-            neg_mean = small.tile([P, 1], F32)
-            nc.vector.tensor_scalar(
-                out=neg_mean[:],
-                in0=sums[:, 0:1],
-                scalar1=sums[:, 1:2],
-                scalar2=-1.0 / HIDDEN,
-                op0=ALU.add,
-                op1=ALU.mult,
-            )
-            squares = work.tile([P, HIDDEN], BF16, bufs=1)
-            sum_squares = small.tile([P, 1], F32)
-            nc.scalar.activation(
-                out=squares[:],
-                in_=x_tiles[q][:, gate * HIDDEN : (gate + 1) * HIDDEN],
-                func=ACT.Square,
-                bias=neg_mean[:],
-                scale=1.0,
-                accum_out=sum_squares[:],
-            )
-            var_eps = small.tile([P, 1], F32)
-            nc.gpsimd.tensor_scalar(
-                out=var_eps[:],
-                in0=sum_squares[:],
-                scalar1=1.0 / HIDDEN,
-                scalar2=EPS,
-                op0=ALU.mult,
-                op1=ALU.add,
-            )
-            rstd = small.tile([P, 1], F32)
-            nc.gpsimd.tensor_tensor(out=rstd[:], in0=var_eps[:], in1=minus_half[:], op=ALU.pow)
-            shift = small.tile([P, 1], F32)
-            nc.gpsimd.tensor_tensor(out=shift[:], in0=neg_mean[:], in1=rstd[:], op=ALU.mult)
-            stats[unit] = (neg_mean, rstd, shift)
 
-        def normalise(unit, x_tiles):
-            gate, q = divmod(unit, SUPER)
-            neg_mean, rstd, shift = stats[unit]
-            lin = x_tiles[q][:, gate * HIDDEN : (gate + 1) * HIDDEN]
-            if q % 2 == 0:
+            w_words = weights.tile([P, PASSES, CHANNELS], U32, align_bytes=64)
+            b_all = weights.tile([P, CHANNELS], BF16)
+            for gate in range(GATES):
+                gate_cols = slice(gate * HIDDEN, (gate + 1) * HIDDEN)
+                gate_bytes = slice(gate * HIDDEN * PACK, (gate + 1) * HIDDEN * PACK)
+                for g in range(PASSES):
+                    nc.sync.dma_start(
+                        out=w_words[:, g, gate_cols].bitcast(I32),
+                        in_=W_words[g].rearrange("p n t -> p (n t)")[:, gate_bytes].bitcast(I32),
+                    )
+                nc.sync.dma_start(out=b_all[:, gate_cols], in_=b[gate_cols].partition_broadcast(P))
+                if gate == 0:
+                    for rt in range(SUPER, ROW_TILES):
+                        nc.sync.dma_start(out=h_raw[:, rt, :], in_=h[rt * P : (rt + 1) * P, :])
+            nc.vector.memset(gn_rows[:], 0.0)
+            nc.sync.dma_start(
+                out=gn_rows[0:gn_pieces, :], in_=gn_weight.rearrange("(t n) -> t n", n=P)
+            )
+            nc.sync.dma_start(
+                out=gn_rows[gn_pieces : 2 * gn_pieces, :],
+                in_=gn_bias.rearrange("(t n) -> t n", n=P),
+            )
+            nc.sync.dma_start(out=c_rows[:], in_=c.rearrange("(r p) n -> p r n", p=P))
+
+            h_codes = weights.tile([P, ROW_TILES, PASSES * P], U32, align_bytes=64)
+            h_scales = weights.tile([P, ROW_TILES, PASSES * P], U8, align_bytes=64)
+            grouped = {}
+
+            def group_h(rt):
+                if not 0 <= rt < ROW_TILES:
+                    return
+                h_pairs = h_raw[:, rt, :].bitcast(F32)
+                h_T = psum.tile([P, BANK], F32, tag="bank")
+                pairs_per_pass = K_PASS // 2
+                for g in range(PASSES):
+                    for u in range(2):
+                        block = 2 * g + u
+                        nc.tensor.transpose(
+                            h_T[:, block * P : (block + 1) * P],
+                            h_pairs[:, pairs_per_pass * g + u : pairs_per_pass * (g + 1) : 2],
+                            ident[:],
+                        )
+                grouped[rt] = stage.tile(
+                    [P, PASSES * P * PACK], BF16, name="grouped", tag="grouped", align_bytes=64
+                )
+                nc.scalar.copy(
+                    out=grouped[rt][:]
+                    .bitcast(F32)
+                    .rearrange("p (g r u) -> p g r u", g=PASSES, u=2),
+                    in_=h_T[:].rearrange("p (g u r) -> p g r u", g=PASSES, u=2),
+                )
+
+            def quantise_h(rt):
+                if not 0 <= rt < ROW_TILES:
+                    return
+                nc.vector.quantize_mx(
+                    out=h_codes[:, rt, :].bitcast(FP8X4),
+                    scales=h_scales[:, rt, :],
+                    in_=grouped[rt][:],
+                )
+
+            stats = {}
+
+            def sum_rows(unit):
+                if not 0 <= unit < UNITS:
+                    return
+                gate, rt = divmod(unit, ROW_TILES)
+                group, col = divmod(unit, GROUP)
+                if col == 0:
+                    stats[("neg_mean", group)] = small.tile([P, GROUP], F32, name="neg_mean")
+                    stats[("sum_squares", group)] = small.tile([P, GROUP], F32, name="sum_squares")
+                neg_mean = stats[("neg_mean", group)][:, col : col + 1]
+                sums = small.tile([P, BANKS_PER_GATE], F32)
+                for half in range(BANKS_PER_GATE):
+                    cols = slice(gate * HIDDEN + half * BANK, gate * HIDDEN + (half + 1) * BANK)
+                    acc = psum.tile([P, BANK], F32, tag="bank")
+                    for g in range(PASSES):
+                        nc.tensor.matmul_mx(
+                            out=acc[:],
+                            lhsT=h_codes[:, rt, g * P : (g + 1) * P].bitcast(FP8X4),
+                            lhsT_scale=h_scales[:, rt, g * P : (g + 1) * P],
+                            rhs=w_words[:, g, cols].bitcast(FP8X4),
+                            rhs_scale=w_planes[4 * g : P, cols],
+                            start=(g == 0),
+                            stop=(g == PASSES - 1),
+                        )
+                    nc.vector.scalar_tensor_tensor(
+                        out=x_rows[:, rt, cols],
+                        in0=acc[:],
+                        scalar=1.0,
+                        in1=b_all[:, cols],
+                        op0=ALU.mult,
+                        op1=ALU.add,
+                        accum_out=sums[:, half : half + 1],
+                    )
                 nc.vector.tensor_scalar(
-                    out=lin,
-                    in0=lin,
-                    scalar1=neg_mean[:],
-                    scalar2=rstd[:],
+                    out=neg_mean,
+                    in0=sums[:, 0:1],
+                    scalar1=sums[:, 1:2],
+                    scalar2=-1.0 / HIDDEN,
                     op0=ALU.add,
                     op1=ALU.mult,
                 )
-            else:
+                squares = stage.tile([P, HIDDEN], BF16, bufs=1)
                 nc.scalar.activation(
-                    out=lin, in_=lin, func=ACT.Identity, scale=rstd[:], bias=shift[:]
+                    out=squares[:],
+                    in_=x_rows[:, rt, gate * HIDDEN : (gate + 1) * HIDDEN],
+                    func=ACT.Square,
+                    bias=neg_mean,
+                    scale=1.0,
+                    accum_out=stats[("sum_squares", group)][:, col : col + 1],
                 )
+                if col == GROUP - 1:
+                    inverse_std(group)
 
-        gn_cols = keep.tile([P, 2 * n_pieces], F32)
+            def inverse_std(group):
+                var_eps = small.tile([P, GROUP], F32)
+                nc.gpsimd.tensor_scalar(
+                    out=var_eps[:],
+                    in0=stats[("sum_squares", group)][:],
+                    scalar1=1.0 / HIDDEN,
+                    scalar2=EPS,
+                    op0=ALU.mult,
+                    op1=ALU.add,
+                )
+                rstd = small.tile([P, GROUP], F32)
+                nc.gpsimd.tensor_tensor(out=rstd[:], in0=var_eps[:], in1=minus_half[:], op=ALU.pow)
+                shift = small.tile([P, GROUP], F32)
+                nc.gpsimd.tensor_tensor(
+                    out=shift[:], in0=stats[("neg_mean", group)][:], in1=rstd[:], op=ALU.mult
+                )
+                stats[("rstd", group)] = rstd
+                stats[("shift", group)] = shift
 
-        def flip_gn_vectors():
+            def normalise(unit):
+                if not 0 <= unit < UNITS:
+                    return
+                gate, rt = divmod(unit, ROW_TILES)
+                group, col = divmod(unit, GROUP)
+                lin = x_rows[:, rt, gate * HIDDEN : (gate + 1) * HIDDEN]
+                rstd = stats[("rstd", group)][:, col : col + 1]
+                if rt % 3 != 1:
+                    nc.vector.tensor_scalar(
+                        out=lin,
+                        in0=lin,
+                        scalar1=stats[("neg_mean", group)][:, col : col + 1],
+                        scalar2=rstd,
+                        op0=ALU.add,
+                        op1=ALU.mult,
+                    )
+                else:
+                    nc.scalar.activation(
+                        out=lin,
+                        in_=lin,
+                        func=ACT.Identity,
+                        scale=rstd,
+                        bias=stats[("shift", group)][:, col : col + 1],
+                    )
+
+            for unit in range(-H_LEAD, UNITS + NORM_LAG):
+                group_h(unit + H_LEAD)
+                quantise_h(unit + H_LEAD - 1)
+                sum_rows(unit)
+                normalise(unit - NORM_LAG)
+
+        with ExitStack() as phase:
+            work = phase.enter_context(tc.tile_pool(name="work", bufs=4))
+
             gn_T = psum.tile([P, P], BF16, tag="bank")
             nc.tensor.transpose(gn_T[:], gn_rows[:], ident_bf16[:])
-            nc.vector.tensor_copy(out=gn_cols[:], in_=gn_T[:, 0 : 2 * n_pieces])
+            nc.vector.tensor_copy(out=gn_cols[:], in_=gn_T[:, 0 : 2 * gn_pieces])
 
-        flipped = {}
+            gate_funcs = {
+                GATE_I: ACT.Sigmoid, GATE_F: ACT.Sigmoid, GATE_O: ACT.Sigmoid, GATE_G: ACT.Tanh
+            }
+            tiles = {}
 
-        def gates(s, j, x_tiles):
-            for gate in range(GATES):
-                first = gate * HIDDEN + j * P
-                x_T = psum.tile([P, BANK], F32, tag="bank")
-                if gate % 2 == 0:
-                    nc.tensor.matmul(
-                        out=x_T[:], lhsT=ident_bf16[:], rhs=c_rows[s][:, 0, 0:BANK],
-                        start=True, stop=True,
-                    )
+            def flip(name, piece, blocks):
+                bank = psum.tile([P, BANK], F32, tag="bank")
                 for q in range(SUPER):
-                    nc.tensor.transpose(
-                        x_T[:, q * P : (q + 1) * P], x_tiles[q][:, first : first + P], ident[:]
+                    nc.tensor.transpose(bank[:, q * P : (q + 1) * P], blocks[q], ident[:])
+                tiles[(name, piece)] = bank
+
+            def gates(piece):
+                if not 0 <= piece < PIECES:
+                    return
+                s, j = divmod(piece, CH_TILES)
+                for gate in range(GATES):
+                    first = gate * HIDDEN + j * P
+                    flip("x", piece, [x_rows[:, s * SUPER + q, first : first + P] for q in range(SUPER)])
+                    t = gate * CH_TILES + j
+                    value = work.tile([P, BANK], F32, name="gate%d" % gate)
+                    nc.scalar.activation(
+                        out=value[:],
+                        in_=tiles[("x", piece)][:],
+                        func=gate_funcs[gate],
+                        scale=gn_cols[:, t : t + 1],
+                        bias=gn_cols[:, gn_pieces + t : gn_pieces + t + 1],
                     )
-                piece = gate * CH_TILES + j
-                value = work.tile([P, BANK], F32, name="gate%d" % gate)
-                nc.scalar.activation(
-                    out=value[:],
-                    in_=x_T[:],
-                    func=gate_funcs[gate],
-                    scale=gn_cols[:, piece : piece + 1],
-                    bias=gn_cols[:, n_pieces + piece : n_pieces + piece + 1],
+                    tiles[(gate, piece)] = value
+
+            def input_product(piece):
+                if not 0 <= piece < PIECES:
+                    return
+                i_T = tiles[(GATE_I, piece)]
+                nc.vector.tensor_mul(out=i_T[:], in0=i_T[:], in1=tiles[(GATE_G, piece)][:])
+
+            def flip_back(name, gate, piece):
+                if not 0 <= piece < PIECES:
+                    return
+                value = tiles[(gate, piece)]
+                flip(name, piece, [value[:, q * P : (q + 1) * P] for q in range(SUPER)])
+
+            def store(value, out, piece):
+                s, j = divmod(piece, CH_TILES)
+                nc.sync.dma_start(
+                    out=out[s * BANK : (s + 1) * BANK, j * P : (j + 1) * P].rearrange(
+                        "(q p) n -> p q n", p=P
+                    ),
+                    in_=value[:],
                 )
-                flipped[("gate", gate, j)] = value
-            c_T = psum.tile([P, BANK], BF16, tag="bank")
-            for q in range(SUPER):
-                nc.tensor.transpose(
-                    c_T[:, q * P : (q + 1) * P], c_rows[s][:, q, j * P : (j + 1) * P], ident_bf16[:]
+
+            def cell(piece):
+                if not 0 <= piece < PIECES:
+                    return
+                s, j = divmod(piece, CH_TILES)
+                kept = work.tile([P, SUPER, P], F32)
+                nc.vector.tensor_mul(
+                    out=kept[:],
+                    in0=tiles[("f_rows", piece)][:].rearrange("p (q n) -> p q n", q=SUPER),
+                    in1=c_rows[:, s * SUPER : (s + 1) * SUPER, j * P : (j + 1) * P],
                 )
-            flipped[("c", j)] = c_T
-
-        def cell(j):
-            i_T = flipped[("gate", 0, j)]
-            f_T = flipped[("gate", 1, j)]
-            g_T = flipped[("gate", 3, j)]
-            nc.vector.tensor_mul(out=f_T[:], in0=f_T[:], in1=flipped[("c", j)][:])
-            nc.vector.tensor_mul(out=i_T[:], in0=i_T[:], in1=g_T[:])
-            c_new_T = work.tile([P, BANK], F32)
-            nc.vector.tensor_add(out=c_new_T[:], in0=f_T[:], in1=i_T[:])
-            flipped[("c_new", j)] = c_new_T
-
-        rows = {}
-
-        def flip_back(name, value_T, j):
-            back = psum.tile([P, BANK], F32, tag="bank")
-            for q in range(SUPER):
-                nc.tensor.transpose(
-                    back[:, q * P : (q + 1) * P], value_T[:, q * P : (q + 1) * P], ident[:]
+                c_new = work.tile([P, SUPER, P], F32)
+                nc.vector.tensor_add(
+                    out=c_new[:],
+                    in0=tiles[("ig_rows", piece)][:].rearrange("p (q n) -> p q n", q=SUPER),
+                    in1=kept[:],
                 )
-            rows[(name, j)] = back
+                store(c_new, out_1, piece)
+                tiles[("c_new", piece)] = c_new
 
-        def tanh_of_cell(j):
-            tanh_c = work.tile([P, BANK], F32)
-            nc.scalar.activation(out=tanh_c[:], in_=rows[("c_new", j)][:], func=ACT.Tanh)
-            rows[("tanh_c", j)] = tanh_c
+            def tanh_of_cell(piece):
+                if not 0 <= piece < PIECES:
+                    return
+                tanh_c = work.tile([P, SUPER, P], F32)
+                nc.scalar.activation(out=tanh_c[:], in_=tiles[("c_new", piece)][:], func=ACT.Tanh)
+                tiles[("tanh_c", piece)] = tanh_c
 
-        def store_rows(value, out, s, j):
-            nc.sync.dma_start(
-                out=out[s * BANK : (s + 1) * BANK, j * P : (j + 1) * P].rearrange(
-                    "(q p) n -> p q n", p=P
-                ),
-                in_=value[:].rearrange("p (q n) -> p q n", q=SUPER),
-            )
+            def hidden(piece):
+                if not 0 <= piece < PIECES:
+                    return
+                h_new = work.tile([P, SUPER, P], F32)
+                nc.vector.tensor_mul(
+                    out=h_new[:],
+                    in0=tiles[("o_rows", piece)][:].rearrange("p (q n) -> p q n", q=SUPER),
+                    in1=tiles[("tanh_c", piece)][:],
+                )
+                store(h_new, out_0, piece)
 
-        def outputs(s, j):
-            c_new = work.tile([P, BANK], F32)
-            nc.vector.tensor_copy(out=c_new[:], in_=rows[("c_new", j)][:])
-            store_rows(c_new, out_1, s, j)
-            h_new = work.tile([P, BANK], F32)
-            nc.vector.tensor_mul(out=h_new[:], in0=rows[("o", j)][:], in1=rows[("tanh_c", j)][:])
-            store_rows(h_new, out_0, s, j)
-
-        quantise_h(0)
-        units = GATES * SUPER
-        for s in range(SUPER_TILES):
-            x_tiles = []
-            for q in range(SUPER):
-                x_tiles.append(normed.tile([P, channels], F32, name="x_rows", tag="x_rows"))
-
-            for unit in range(units + NORM_LAG):
-                if unit < units:
-                    sum_rows(s, unit, x_tiles)
-                if unit >= NORM_LAG:
-                    normalise(unit - NORM_LAG, x_tiles)
-
-            if s == 0:
-                flip_gn_vectors()
-            if s + 1 < SUPER_TILES:
-                quantise_h(s + 1)
-
-            for j in range(CH_TILES + 2):
-                if j >= 2:
-                    tanh_of_cell(j - 2)
-                if j < CH_TILES:
-                    gates(s, j, x_tiles)
-                if 1 <= j <= CH_TILES:
-                    cell(j - 1)
-                    flip_back("c_new", flipped[("c_new", j - 1)], j - 1)
-                    flip_back("o", flipped[("gate", 2, j - 1)], j - 1)
-                if j >= 2:
-                    outputs(s, j - 2)
+            for piece in range(PIECES + 3):
+                input_product(piece - 1)
+                hidden(piece - 3)
+                cell(piece - 2)
+                gates(piece)
+                tanh_of_cell(piece - 2)
+                flip_back("f_rows", GATE_F, piece - 1)
+                flip_back("ig_rows", GATE_I, piece - 1)
+                flip_back("o_rows", GATE_O, piece - 2)

@@ -29,7 +29,7 @@ EPS = 1e-5
 UNITS = GATES * ROW_TILES
 H_LEAD = 2
 GROUP = 4
-NORM_LAG = 2 * GROUP
+NORM_LAG = GROUP
 
 SUPER = BANK // P
 CH_TILES = HIDDEN // P
@@ -213,12 +213,7 @@ def tile_lstmcell2_kernel(
                 )
                 rstd = small.tile([P, GROUP], F32)
                 nc.gpsimd.tensor_tensor(out=rstd[:], in0=var_eps[:], in1=minus_half[:], op=ALU.pow)
-                shift = small.tile([P, GROUP], F32)
-                nc.gpsimd.tensor_tensor(
-                    out=shift[:], in0=stats[("neg_mean", group)][:], in1=rstd[:], op=ALU.mult
-                )
                 stats[("rstd", group)] = rstd
-                stats[("shift", group)] = shift
 
             def normalise(unit):
                 if not 0 <= unit < UNITS:
@@ -227,29 +222,20 @@ def tile_lstmcell2_kernel(
                 group, col = divmod(unit, GROUP)
                 lin = x_rows[:, rt, gate * HIDDEN : (gate + 1) * HIDDEN]
                 rstd = stats[("rstd", group)][:, col : col + 1]
-                if rt % 3 != 1:
-                    nc.vector.tensor_scalar(
-                        out=lin,
-                        in0=lin,
-                        scalar1=stats[("neg_mean", group)][:, col : col + 1],
-                        scalar2=rstd,
-                        op0=ALU.add,
-                        op1=ALU.mult,
-                    )
-                else:
-                    nc.scalar.activation(
-                        out=lin,
-                        in_=lin,
-                        func=ACT.Identity,
-                        scale=rstd,
-                        bias=stats[("shift", group)][:, col : col + 1],
-                    )
+                nc.gpsimd.tensor_scalar(
+                    out=lin,
+                    in0=lin,
+                    scalar1=stats[("neg_mean", group)][:, col : col + 1],
+                    scalar2=rstd,
+                    op0=ALU.add,
+                    op1=ALU.mult,
+                )
 
             for unit in range(-H_LEAD, UNITS + NORM_LAG):
                 group_h(unit + H_LEAD)
                 quantise_h(unit + H_LEAD - 1)
-                sum_rows(unit)
                 normalise(unit - NORM_LAG)
+                sum_rows(unit)
 
         with ExitStack() as phase:
             work = phase.enter_context(tc.tile_pool(name="work", bufs=4))

@@ -29,7 +29,7 @@ EPS = 1e-5
 UNITS = GATES * ROW_TILES
 H_LEAD = 2
 GROUP = 4
-NORM_LAG = GROUP
+NORM_LAG = GROUP + 1
 
 SUPER = BANK // P
 CH_TILES = HIDDEN // P
@@ -61,8 +61,8 @@ def tile_lstmcell2_kernel(
         make_identity(nc, ident[:])
         ident_bf16 = keep.tile([P, P], BF16)
         make_identity(nc, ident_bf16[:])
-        minus_half = keep.tile([P, GROUP], F32)
-        nc.gpsimd.memset(minus_half[:], -0.5)
+        eps_col = keep.tile([P, 1], F32)
+        nc.gpsimd.memset(eps_col[:], EPS)
 
         x_rows = keep.tile([P, ROW_TILES, CHANNELS], F32)
         c_rows = keep.tile([P, ROW_TILES, HIDDEN], BF16)
@@ -149,71 +149,79 @@ def tile_lstmcell2_kernel(
 
             stats = {}
 
-            def sum_rows(unit):
+            def add_bias(unit, half):
                 if not 0 <= unit < UNITS:
                     return
                 gate, rt = divmod(unit, ROW_TILES)
                 group, col = divmod(unit, GROUP)
-                if col == 0:
+                if col == 0 and half == 0:
                     stats[("neg_mean", group)] = small.tile([P, GROUP], F32, name="neg_mean")
                     stats[("sum_squares", group)] = small.tile([P, GROUP], F32, name="sum_squares")
-                neg_mean = stats[("neg_mean", group)][:, col : col + 1]
-                sums = small.tile([P, BANKS_PER_GATE], F32)
-                for half in range(BANKS_PER_GATE):
-                    cols = slice(gate * HIDDEN + half * BANK, gate * HIDDEN + (half + 1) * BANK)
-                    acc = psum.tile([P, BANK], F32, tag="bank")
-                    for g in range(PASSES):
-                        nc.tensor.matmul_mx(
-                            out=acc[:],
-                            lhsT=h_codes[:, rt, g * P : (g + 1) * P].bitcast(FP8X4),
-                            lhsT_scale=h_scales[:, rt, g * P : (g + 1) * P],
-                            rhs=w_words[:, g, cols].bitcast(FP8X4),
-                            rhs_scale=w_planes[4 * g : P, cols],
-                            start=(g == 0),
-                            stop=(g == PASSES - 1),
-                        )
-                    nc.vector.scalar_tensor_tensor(
-                        out=x_rows[:, rt, cols],
-                        in0=acc[:],
-                        scalar=1.0,
-                        in1=b_all[:, cols],
-                        op0=ALU.mult,
-                        op1=ALU.add,
-                        accum_out=sums[:, half : half + 1],
+                    stats[("rstd", group)] = small.tile([P, GROUP], F32, name="rstd")
+                if half == 0:
+                    stats[("sums", unit)] = small.tile([P, BANKS_PER_GATE], F32, name="sums")
+                cols = slice(gate * HIDDEN + half * BANK, gate * HIDDEN + (half + 1) * BANK)
+                acc = psum.tile([P, BANK], F32, tag="bank")
+                for g in range(PASSES):
+                    nc.tensor.matmul_mx(
+                        out=acc[:],
+                        lhsT=h_codes[:, rt, g * P : (g + 1) * P].bitcast(FP8X4),
+                        lhsT_scale=h_scales[:, rt, g * P : (g + 1) * P],
+                        rhs=w_words[:, g, cols].bitcast(FP8X4),
+                        rhs_scale=w_planes[4 * g : P, cols],
+                        start=(g == 0),
+                        stop=(g == PASSES - 1),
                     )
+                nc.vector.scalar_tensor_tensor(
+                    out=x_rows[:, rt, cols],
+                    in0=acc[:],
+                    scalar=1.0,
+                    in1=b_all[:, cols],
+                    op0=ALU.mult,
+                    op1=ALU.add,
+                    accum_out=stats[("sums", unit)][:, half : half + 1],
+                )
+
+            def mean_of(unit):
+                if not 0 <= unit < UNITS:
+                    return
+                group, col = divmod(unit, GROUP)
+                sums = stats[("sums", unit)]
                 nc.vector.tensor_scalar(
-                    out=neg_mean,
+                    out=stats[("neg_mean", group)][:, col : col + 1],
                     in0=sums[:, 0:1],
                     scalar1=sums[:, 1:2],
                     scalar2=-1.0 / HIDDEN,
                     op0=ALU.add,
                     op1=ALU.mult,
                 )
+
+            def square(unit):
+                if not 0 <= unit < UNITS:
+                    return
+                gate, rt = divmod(unit, ROW_TILES)
+                group, col = divmod(unit, GROUP)
                 squares = stage.tile([P, HIDDEN], BF16, bufs=1)
                 nc.scalar.activation(
                     out=squares[:],
                     in_=x_rows[:, rt, gate * HIDDEN : (gate + 1) * HIDDEN],
                     func=ACT.Square,
-                    bias=neg_mean,
+                    bias=stats[("neg_mean", group)][:, col : col + 1],
                     scale=1.0,
                     accum_out=stats[("sum_squares", group)][:, col : col + 1],
                 )
-                if col == GROUP - 1:
-                    inverse_std(group)
 
-            def inverse_std(group):
-                var_eps = small.tile([P, GROUP], F32)
-                nc.gpsimd.tensor_scalar(
-                    out=var_eps[:],
-                    in0=stats[("sum_squares", group)][:],
-                    scalar1=1.0 / HIDDEN,
-                    scalar2=EPS,
-                    op0=ALU.mult,
-                    op1=ALU.add,
+            def inverse_std(unit):
+                if not 0 <= unit < UNITS or unit % GROUP != GROUP - 1:
+                    return
+                group = unit // GROUP
+                nc.scalar.activation(
+                    out=stats[("rstd", group)][:],
+                    in_=stats[("sum_squares", group)][:],
+                    func=ACT.Abs_reciprocal_sqrt,
+                    scale=1.0 / HIDDEN,
+                    bias=eps_col[:],
                 )
-                rstd = small.tile([P, GROUP], F32)
-                nc.gpsimd.tensor_tensor(out=rstd[:], in0=var_eps[:], in1=minus_half[:], op=ALU.pow)
-                stats[("rstd", group)] = rstd
 
             def normalise(unit):
                 if not 0 <= unit < UNITS:
@@ -221,12 +229,11 @@ def tile_lstmcell2_kernel(
                 gate, rt = divmod(unit, ROW_TILES)
                 group, col = divmod(unit, GROUP)
                 lin = x_rows[:, rt, gate * HIDDEN : (gate + 1) * HIDDEN]
-                rstd = stats[("rstd", group)][:, col : col + 1]
                 nc.gpsimd.tensor_scalar(
                     out=lin,
                     in0=lin,
                     scalar1=stats[("neg_mean", group)][:, col : col + 1],
-                    scalar2=rstd,
+                    scalar2=stats[("rstd", group)][:, col : col + 1],
                     op0=ALU.add,
                     op1=ALU.mult,
                 )
@@ -234,8 +241,12 @@ def tile_lstmcell2_kernel(
             for unit in range(-H_LEAD, UNITS + NORM_LAG):
                 group_h(unit + H_LEAD)
                 quantise_h(unit + H_LEAD - 1)
+                add_bias(unit, 0)
+                mean_of(unit - 1)
+                add_bias(unit, 1)
+                square(unit - 1)
+                inverse_std(unit - 2)
                 normalise(unit - NORM_LAG)
-                sum_rows(unit)
 
         with ExitStack() as phase:
             work = phase.enter_context(tc.tile_pool(name="work", bufs=4))

@@ -174,9 +174,9 @@ def tile_lstmcell2_kernel(
                     )
                 nc.vector.scalar_tensor_tensor(
                     out=x_rows[:, rt, cols],
-                    in0=acc[:],
+                    in0=b_all[:, cols],
                     scalar=1.0,
-                    in1=b_all[:, cols],
+                    in1=acc[:],
                     op0=ALU.mult,
                     op1=ALU.add,
                     accum_out=stats[("sums", unit)][:, half : half + 1],
@@ -187,13 +187,15 @@ def tile_lstmcell2_kernel(
                     return
                 group, col = divmod(unit, GROUP)
                 sums = stats[("sums", unit)]
+                scaled = small.tile([P, BANKS_PER_GATE], F32)
                 nc.vector.tensor_scalar(
-                    out=stats[("neg_mean", group)][:, col : col + 1],
-                    in0=sums[:, 0:1],
-                    scalar1=sums[:, 1:2],
-                    scalar2=-1.0 / HIDDEN,
-                    op0=ALU.add,
-                    op1=ALU.mult,
+                    out=scaled[:],
+                    in0=sums[:],
+                    scalar1=-1.0 / HIDDEN,
+                    scalar2=None,
+                    op0=ALU.mult,
+                    op1=ALU.add,
+                    accum_out=stats[("neg_mean", group)][:, col : col + 1],
                 )
 
             def square(unit):

@@ -97,9 +97,8 @@ def tile_lstmcell2_kernel(
                         in_=W_words[g].rearrange("p n t -> p (n t)")[:, gate_bytes].bitcast(I32),
                     )
                 nc.sync.dma_start(out=b_all[:, gate_cols], in_=b[gate_cols].partition_broadcast(P))
-                if gate == 0:
-                    for rt in range(SUPER, ROW_TILES):
-                        nc.sync.dma_start(out=h_raw[:, rt, :], in_=h[rt * P : (rt + 1) * P, :])
+            for rt in range(SUPER, ROW_TILES):
+                nc.sync.dma_start(out=h_raw[:, rt, :], in_=h[rt * P : (rt + 1) * P, :])
             nc.vector.memset(gn_rows[:], 0.0)
             nc.sync.dma_start(
                 out=gn_rows[0:gn_pieces, :], in_=gn_weight.rearrange("(t n) -> t n", n=P)
@@ -149,10 +148,20 @@ def tile_lstmcell2_kernel(
 
             stats = {}
 
+            def place(unit):
+                s, rest = divmod(unit, GATES * SUPER)
+                gate, q = divmod(rest, SUPER)
+                return gate, s * SUPER + q
+
+            def new_row_tile(unit):
+                if not 0 <= unit < UNITS or unit % (GATES * SUPER) >= SUPER:
+                    return -1
+                return place(unit)[1]
+
             def add_bias(unit, half):
                 if not 0 <= unit < UNITS:
                     return
-                gate, rt = divmod(unit, ROW_TILES)
+                gate, rt = place(unit)
                 group, col = divmod(unit, GROUP)
                 if col == 0 and half == 0:
                     stats[("neg_mean", group)] = small.tile([P, GROUP], F32, name="neg_mean")
@@ -201,7 +210,7 @@ def tile_lstmcell2_kernel(
             def square(unit):
                 if not 0 <= unit < UNITS:
                     return
-                gate, rt = divmod(unit, ROW_TILES)
+                gate, rt = place(unit)
                 group, col = divmod(unit, GROUP)
                 squares = stage.tile([P, HIDDEN], BF16, bufs=1)
                 nc.scalar.activation(
@@ -225,13 +234,11 @@ def tile_lstmcell2_kernel(
                     bias=eps_col[:],
                 )
 
-            def normalise(unit):
-                if not 0 <= unit < UNITS:
-                    return
-                gate, rt = divmod(unit, ROW_TILES)
+            def normalise(engine, unit):
+                gate, rt = place(unit)
                 group, col = divmod(unit, GROUP)
                 lin = x_rows[:, rt, gate * HIDDEN : (gate + 1) * HIDDEN]
-                nc.gpsimd.tensor_scalar(
+                engine.tensor_scalar(
                     out=lin,
                     in0=lin,
                     scalar1=stats[("neg_mean", group)][:, col : col + 1],
@@ -240,22 +247,25 @@ def tile_lstmcell2_kernel(
                     op1=ALU.mult,
                 )
 
-            for unit in range(-H_LEAD, UNITS + NORM_LAG):
-                group_h(unit + H_LEAD)
-                quantise_h(unit + H_LEAD - 1)
+            for unit in range(-H_LEAD, UNITS + 3):
+                group_h(new_row_tile(unit + H_LEAD))
+                quantise_h(new_row_tile(unit + H_LEAD - 1))
                 add_bias(unit, 0)
                 mean_of(unit - 1)
                 add_bias(unit, 1)
                 square(unit - 1)
                 inverse_std(unit - 2)
-                normalise(unit - NORM_LAG)
-
-        with ExitStack() as phase:
-            work = phase.enter_context(tc.tile_pool(name="work", bufs=4))
-
+                if 0 <= unit - NORM_LAG < UNITS // 2:
+                    normalise(nc.gpsimd, unit - NORM_LAG)
             gn_T = psum.tile([P, P], BF16, tag="bank")
             nc.tensor.transpose(gn_T[:], gn_rows[:], ident_bf16[:])
             nc.vector.tensor_copy(out=gn_cols[:], in_=gn_T[:, 0 : 2 * gn_pieces])
+
+            for unit in range(UNITS // 2, UNITS):
+                normalise(nc.vector, unit)
+
+        with ExitStack() as phase:
+            work = phase.enter_context(tc.tile_pool(name="work", bufs=4))
 
             gate_funcs = {
                 GATE_I: ACT.Sigmoid, GATE_F: ACT.Sigmoid, GATE_O: ACT.Sigmoid, GATE_G: ACT.Tanh

@@ -278,23 +278,30 @@ def tile_lstmcell2_kernel(
                     nc.tensor.transpose(bank[:, q * P : (q + 1) * P], blocks[q], ident[:])
                 tiles[(name, piece)] = bank
 
-            def gates(piece):
+            def flip_gate(gate, piece):
                 if not 0 <= piece < PIECES:
                     return
                 s, j = divmod(piece, CH_TILES)
-                for gate in range(GATES):
-                    first = gate * HIDDEN + j * P
-                    flip("x", piece, [x_rows[:, s * SUPER + q, first : first + P] for q in range(SUPER)])
-                    t = gate * CH_TILES + j
-                    value = work.tile([P, BANK], F32, name="gate%d" % gate)
-                    nc.scalar.activation(
-                        out=value[:],
-                        in_=tiles[("x", piece)][:],
-                        func=gate_funcs[gate],
-                        scale=gn_cols[:, t : t + 1],
-                        bias=gn_cols[:, gn_pieces + t : gn_pieces + t + 1],
-                    )
-                    tiles[(gate, piece)] = value
+                first = gate * HIDDEN + j * P
+                flip(
+                    ("x", gate),
+                    piece,
+                    [x_rows[:, s * SUPER + q, first : first + P] for q in range(SUPER)],
+                )
+
+            def activate(gate, piece):
+                if not 0 <= piece < PIECES:
+                    return
+                t = gate * CH_TILES + piece % CH_TILES
+                value = work.tile([P, BANK], F32, name="gate%d" % gate)
+                nc.scalar.activation(
+                    out=value[:],
+                    in_=tiles[(("x", gate), piece)][:],
+                    func=gate_funcs[gate],
+                    scale=gn_cols[:, t : t + 1],
+                    bias=gn_cols[:, gn_pieces + t : gn_pieces + t + 1],
+                )
+                tiles[(gate, piece)] = value
 
             def input_product(piece):
                 if not 0 <= piece < PIECES:
@@ -317,7 +324,7 @@ def tile_lstmcell2_kernel(
                     in_=value[:],
                 )
 
-            def cell(piece):
+            def keep_part(piece):
                 if not 0 <= piece < PIECES:
                     return
                 s, j = divmod(piece, CH_TILES)
@@ -327,11 +334,16 @@ def tile_lstmcell2_kernel(
                     in0=tiles[("f_rows", piece)][:].rearrange("p (q n) -> p q n", q=SUPER),
                     in1=c_rows[:, s * SUPER : (s + 1) * SUPER, j * P : (j + 1) * P],
                 )
+                tiles[("kept", piece)] = kept
+
+            def new_cell(piece):
+                if not 0 <= piece < PIECES:
+                    return
                 c_new = work.tile([P, SUPER, P], F32)
                 nc.vector.tensor_add(
                     out=c_new[:],
                     in0=tiles[("ig_rows", piece)][:].rearrange("p (q n) -> p q n", q=SUPER),
-                    in1=kept[:],
+                    in1=tiles[("kept", piece)][:],
                 )
                 store(c_new, out_1, piece)
                 tiles[("c_new", piece)] = c_new
@@ -354,12 +366,21 @@ def tile_lstmcell2_kernel(
                 )
                 store(h_new, out_0, piece)
 
-            for piece in range(PIECES + 3):
-                input_product(piece - 1)
-                hidden(piece - 3)
-                cell(piece - 2)
-                gates(piece)
-                tanh_of_cell(piece - 2)
-                flip_back("f_rows", GATE_F, piece - 1)
-                flip_back("ig_rows", GATE_I, piece - 1)
-                flip_back("o_rows", GATE_O, piece - 2)
+            flip_gate(GATE_I, 0)
+            for piece in range(PIECES + 2):
+                flip_gate(GATE_G, piece)
+                flip_gate(GATE_F, piece)
+                flip_gate(GATE_O, piece)
+                hidden(piece - 2)
+                new_cell(piece - 1)
+                activate(GATE_I, piece)
+                activate(GATE_G, piece)
+                activate(GATE_F, piece)
+                activate(GATE_O, piece)
+                tanh_of_cell(piece - 1)
+                flip_back("o_rows", GATE_O, piece - 1)
+                flip_gate(GATE_I, piece + 1)
+                input_product(piece)
+                flip_back("f_rows", GATE_F, piece)
+                flip_back("ig_rows", GATE_I, piece)
+                keep_part(piece)

@@ -61,8 +61,8 @@ def tile_lstmcell2_kernel(
         make_identity(nc, ident[:])
         ident_bf16 = keep.tile([P, P], BF16)
         make_identity(nc, ident_bf16[:])
-        eps_col = keep.tile([P, 1], F32)
-        nc.gpsimd.memset(eps_col[:], EPS)
+        minus_half = keep.tile([P, GROUP], F32)
+        nc.gpsimd.memset(minus_half[:], -0.5)
 
         x_rows = keep.tile([P, ROW_TILES, CHANNELS], F32)
         c_rows = keep.tile([P, ROW_TILES, HIDDEN], BF16)
@@ -226,12 +226,17 @@ def tile_lstmcell2_kernel(
                 if not 0 <= unit < UNITS or unit % GROUP != GROUP - 1:
                     return
                 group = unit // GROUP
-                nc.scalar.activation(
-                    out=stats[("rstd", group)][:],
-                    in_=stats[("sum_squares", group)][:],
-                    func=ACT.Abs_reciprocal_sqrt,
-                    scale=1.0 / HIDDEN,
-                    bias=eps_col[:],
+                var_eps = small.tile([P, GROUP], F32)
+                nc.gpsimd.tensor_scalar(
+                    out=var_eps[:],
+                    in0=stats[("sum_squares", group)][:],
+                    scalar1=1.0 / HIDDEN,
+                    scalar2=EPS,
+                    op0=ALU.mult,
+                    op1=ALU.add,
+                )
+                nc.gpsimd.tensor_tensor(
+                    out=stats[("rstd", group)][:], in0=var_eps[:], in1=minus_half[:], op=ALU.pow
                 )
 
             def normalise(engine, unit):
@@ -247,7 +252,7 @@ def tile_lstmcell2_kernel(
                     op1=ALU.mult,
                 )
 
-            for unit in range(-H_LEAD, UNITS + 3):
+            for unit in range(-H_LEAD, UNITS + NORM_LAG):
                 group_h(new_row_tile(unit + H_LEAD))
                 quantise_h(new_row_tile(unit + H_LEAD - 1))
                 add_bias(unit, 0)
@@ -255,14 +260,12 @@ def tile_lstmcell2_kernel(
                 add_bias(unit, 1)
                 square(unit - 1)
                 inverse_std(unit - 2)
-                if 0 <= unit - NORM_LAG < UNITS // 2:
+                if 0 <= unit - NORM_LAG < UNITS:
                     normalise(nc.gpsimd, unit - NORM_LAG)
             gn_T = psum.tile([P, P], BF16, tag="bank")
             nc.tensor.transpose(gn_T[:], gn_rows[:], ident_bf16[:])
             nc.vector.tensor_copy(out=gn_cols[:], in_=gn_T[:, 0 : 2 * gn_pieces])
 
-            for unit in range(UNITS // 2, UNITS):
-                normalise(nc.vector, unit)
 
         with ExitStack() as phase:
             work = phase.enter_context(tc.tile_pool(name="work", bufs=4))
@@ -366,21 +369,22 @@ def tile_lstmcell2_kernel(
                 )
                 store(h_new, out_0, piece)
 
-            flip_gate(GATE_I, 0)
+            for gate in (GATE_I, GATE_G, GATE_F, GATE_O):
+                flip_gate(gate, 0)
             for piece in range(PIECES + 2):
-                flip_gate(GATE_G, piece)
-                flip_gate(GATE_F, piece)
-                flip_gate(GATE_O, piece)
+                flip_back("o_rows", GATE_O, piece - 1)
                 hidden(piece - 2)
                 new_cell(piece - 1)
                 activate(GATE_I, piece)
-                activate(GATE_G, piece)
-                activate(GATE_F, piece)
-                activate(GATE_O, piece)
-                tanh_of_cell(piece - 1)
-                flip_back("o_rows", GATE_O, piece - 1)
                 flip_gate(GATE_I, piece + 1)
+                activate(GATE_G, piece)
+                flip_gate(GATE_G, piece + 1)
                 input_product(piece)
+                activate(GATE_F, piece)
+                flip_gate(GATE_F, piece + 1)
                 flip_back("f_rows", GATE_F, piece)
                 flip_back("ig_rows", GATE_I, piece)
+                activate(GATE_O, piece)
+                flip_gate(GATE_O, piece + 1)
+                tanh_of_cell(piece - 1)
                 keep_part(piece)

@@ -158,6 +158,33 @@ def tile_lstmcell2_kernel(
                     return -1
                 return place(unit)[1]
 
+            def last_units(unit):
+                return unit >= UNITS - 2
+
+            def statistics_on_vector(unit):
+                gate, rt = place(unit)
+                group, col = divmod(unit, GROUP)
+                parts = small.tile([P, BANKS_PER_GATE, 6], F32)
+                for half in range(BANKS_PER_GATE):
+                    first = gate * HIDDEN + half * BANK
+                    nc.vector.bn_stats(out=parts[:, half, :], in_=x_rows[:, rt, first : first + BANK])
+                mean_var = small.tile([P, 2], F32)
+                nc.vector.bn_aggr(out=mean_var[:], in_=parts[:].rearrange("p a s -> p (a s)"))
+                nc.vector.tensor_scalar(
+                    out=stats[("neg_mean", group)][:, col : col + 1],
+                    in0=mean_var[:, 0:1],
+                    scalar1=-1.0,
+                    scalar2=None,
+                    op0=ALU.mult,
+                )
+                nc.vector.tensor_scalar(
+                    out=stats[("sum_squares", group)][:, col : col + 1],
+                    in0=mean_var[:, 1:2],
+                    scalar1=float(HIDDEN),
+                    scalar2=None,
+                    op0=ALU.mult,
+                )
+
             def add_bias(unit, half):
                 if not 0 <= unit < UNITS:
                     return
@@ -188,11 +215,11 @@ def tile_lstmcell2_kernel(
                     in1=acc[:],
                     op0=ALU.mult,
                     op1=ALU.add,
-                    accum_out=stats[("sums", unit)][:, half : half + 1],
+                    accum_out=None if last_units(unit) else stats[("sums", unit)][:, half : half + 1],
                 )
 
             def mean_of(unit):
-                if not 0 <= unit < UNITS:
+                if not 0 <= unit < UNITS or last_units(unit):
                     return
                 group, col = divmod(unit, GROUP)
                 sums = stats[("sums", unit)]
@@ -208,7 +235,7 @@ def tile_lstmcell2_kernel(
                 )
 
             def square(unit):
-                if not 0 <= unit < UNITS:
+                if not 0 <= unit < UNITS or last_units(unit):
                     return
                 gate, rt = place(unit)
                 group, col = divmod(unit, GROUP)
@@ -254,18 +281,21 @@ def tile_lstmcell2_kernel(
 
             for unit in range(-H_LEAD, UNITS + NORM_LAG):
                 group_h(new_row_tile(unit + H_LEAD))
+                if unit + H_LEAD == UNITS // 2:
+                    gn_T = psum.tile([P, P], BF16, tag="bank")
+                    nc.tensor.transpose(gn_T[:], gn_rows[:], ident_bf16[:])
+                    nc.vector.tensor_copy(out=gn_cols[:], in_=gn_T[:, 0 : 2 * gn_pieces])
                 quantise_h(new_row_tile(unit + H_LEAD - 1))
                 add_bias(unit, 0)
                 mean_of(unit - 1)
                 add_bias(unit, 1)
+                if unit == UNITS - 1:
+                    statistics_on_vector(UNITS - 2)
+                    statistics_on_vector(UNITS - 1)
                 square(unit - 1)
                 inverse_std(unit - 2)
                 if 0 <= unit - NORM_LAG < UNITS:
                     normalise(nc.gpsimd, unit - NORM_LAG)
-            gn_T = psum.tile([P, P], BF16, tag="bank")
-            nc.tensor.transpose(gn_T[:], gn_rows[:], ident_bf16[:])
-            nc.vector.tensor_copy(out=gn_cols[:], in_=gn_T[:, 0 : 2 * gn_pieces])
-
 
         with ExitStack() as phase:
             work = phase.enter_context(tc.tile_pool(name="work", bufs=4))
@@ -381,8 +411,8 @@ def tile_lstmcell2_kernel(
                 flip_gate(GATE_G, piece + 1)
                 input_product(piece)
                 activate(GATE_F, piece)
-                flip_gate(GATE_F, piece + 1)
                 flip_back("f_rows", GATE_F, piece)
+                flip_gate(GATE_F, piece + 1)
                 flip_back("ig_rows", GATE_I, piece)
                 activate(GATE_O, piece)
                 flip_gate(GATE_O, piece + 1)

@@ -19,6 +19,7 @@ BATCH = 1024
 HIDDEN = 1024
 GATES = 4
 GATE_I, GATE_F, GATE_O, GATE_G = 0, 1, 2, 3
+GATE_ORDER = (GATE_I, GATE_G, GATE_F, GATE_O)
 CHANNELS = GATES * HIDDEN
 PASSES = HIDDEN // K_PASS
 ROW_TILES = BATCH // P
@@ -88,7 +89,7 @@ def tile_lstmcell2_kernel(
 
             w_words = weights.tile([P, PASSES, CHANNELS], U32, align_bytes=64)
             b_all = weights.tile([P, CHANNELS], BF16)
-            for gate in range(GATES):
+            for gate in GATE_ORDER:
                 gate_cols = slice(gate * HIDDEN, (gate + 1) * HIDDEN)
                 gate_bytes = slice(gate * HIDDEN * PACK, (gate + 1) * HIDDEN * PACK)
                 for g in range(PASSES):
@@ -128,7 +129,7 @@ def tile_lstmcell2_kernel(
                             ident[:],
                         )
                 grouped[rt] = stage.tile(
-                    [P, PASSES * P * PACK], BF16, name="grouped", tag="grouped", align_bytes=64
+                    [P, PASSES * P * PACK], BF16, name="grouped", tag="grouped", align_bytes=64, bufs=SUPER
                 )
                 nc.scalar.copy(
                     out=grouped[rt][:]
@@ -150,8 +151,8 @@ def tile_lstmcell2_kernel(
 
             def place(unit):
                 s, rest = divmod(unit, GATES * SUPER)
-                gate, q = divmod(rest, SUPER)
-                return gate, s * SUPER + q
+                turn, q = divmod(rest, SUPER)
+                return GATE_ORDER[turn], s * SUPER + q
 
             def new_row_tile(unit):
                 if not 0 <= unit < UNITS or unit % (GATES * SUPER) >= SUPER:
@@ -223,15 +224,13 @@ def tile_lstmcell2_kernel(
                     return
                 group, col = divmod(unit, GROUP)
                 sums = stats[("sums", unit)]
-                scaled = small.tile([P, BANKS_PER_GATE], F32)
                 nc.vector.tensor_scalar(
-                    out=scaled[:],
-                    in0=sums[:],
-                    scalar1=-1.0 / HIDDEN,
-                    scalar2=None,
-                    op0=ALU.mult,
-                    op1=ALU.add,
-                    accum_out=stats[("neg_mean", group)][:, col : col + 1],
+                    out=stats[("neg_mean", group)][:, col : col + 1],
+                    in0=sums[:, 0:1],
+                    scalar1=sums[:, 1:2],
+                    scalar2=-1.0 / HIDDEN,
+                    op0=ALU.add,
+                    op1=ALU.mult,
                 )
 
             def square(unit):
@@ -280,7 +279,10 @@ def tile_lstmcell2_kernel(
                 )
 
             for unit in range(-H_LEAD, UNITS + NORM_LAG):
-                group_h(new_row_tile(unit + H_LEAD))
+                ahead = new_row_tile(unit + H_LEAD)
+                if ahead >= 0 and ahead % SUPER == 0:
+                    for rt in range(ahead, ahead + SUPER):
+                        group_h(rt)
                 if unit + H_LEAD == UNITS // 2:
                     gn_T = psum.tile([P, P], BF16, tag="bank")
                     nc.tensor.transpose(gn_T[:], gn_rows[:], ident_bf16[:])
@@ -399,7 +401,7 @@ def tile_lstmcell2_kernel(
                 )
                 store(h_new, out_0, piece)
 
-            for gate in (GATE_I, GATE_G, GATE_F, GATE_O):
+            for gate in GATE_ORDER:
                 flip_gate(gate, 0)
             for piece in range(PIECES + 2):
                 flip_back("o_rows", GATE_O, piece - 1)

from contextlib import ExitStack

import concourse.mybir as mybir
from concourse.masks import make_identity

F32 = mybir.dt.float32
BF16 = mybir.dt.bfloat16
I32 = mybir.dt.int32
U32 = mybir.dt.uint32
U8 = mybir.dt.uint8
FP8X4 = mybir.dt.float8_e4m3fn_x4
ALU = mybir.AluOpType
ACT = mybir.ActivationFunctionType

P = 128
PACK = 4
K_PASS = P * PACK
BATCH = 1024
HIDDEN = 1024
GATES = 4
GATE_I, GATE_F, GATE_O, GATE_G = 0, 1, 2, 3
GATE_ORDER = (GATE_I, GATE_G, GATE_F, GATE_O)
CHANNELS = GATES * HIDDEN
PASSES = HIDDEN // K_PASS
ROW_TILES = BATCH // P
BANK = 512
BANKS_PER_GATE = HIDDEN // BANK
EPS = 1e-5

UNITS = GATES * ROW_TILES
H_LEAD = 2
GROUP = 4
NORM_LAG = GROUP + 1

SUPER = BANK // P
CH_TILES = HIDDEN // P
PIECES = (ROW_TILES // SUPER) * CH_TILES

FLOPS = 2 * BATCH * HIDDEN * CHANNELS
BYTES = (
    2 * BATCH * HIDDEN * 2
    + HIDDEN * CHANNELS
    + HIDDEN // 32 * CHANNELS
    + 3 * CHANNELS * 2
    + 2 * BATCH * HIDDEN * 4
)


def tile_lstmcell2_kernel(
    tc, x, h, c, W_words, W_scales, b, gn_weight, gn_bias, out_0, out_1
):
    nc = tc.nc
    gn_pieces = CHANNELS // P

    with ExitStack() as whole:
        whole.enter_context(tc.manual_schedule())
        keep = whole.enter_context(tc.tile_pool(name="keep", bufs=1))
        small = whole.enter_context(tc.tile_pool(name="small", bufs=4))
        psum = whole.enter_context(tc.psum_pool(name="psum", bufs=8))

        ident = keep.tile([P, P], F32)
        make_identity(nc, ident[:])
        ident_bf16 = keep.tile([P, P], BF16)
        make_identity(nc, ident_bf16[:])
        minus_half = keep.tile([P, GROUP], F32)
        nc.gpsimd.memset(minus_half[:], -0.5)

        x_rows = keep.tile([P, ROW_TILES, CHANNELS], F32)
        c_rows = keep.tile([P, ROW_TILES, HIDDEN], BF16)
        gn_rows = keep.tile([P, P], BF16)
        gn_cols = keep.tile([P, 2 * gn_pieces], F32)

        with ExitStack() as phase:
            weights = phase.enter_context(tc.tile_pool(name="weights", bufs=1))
            stage = phase.enter_context(tc.tile_pool(name="stage", bufs=3))

            h_raw = weights.tile([P, ROW_TILES, HIDDEN], BF16)
            for rt in range(SUPER):
                nc.scalar.dma_start(out=h_raw[:, rt, :], in_=h[rt * P : (rt + 1) * P, :])

            w_planes = weights.tile([P, CHANNELS], U8, align_bytes=64)
            nc.vector.memset(w_planes[:].bitcast(I32), 0)
            scale_words = W_scales.bitcast(I32)
            for quad in range(4):
                nc.sync.dma_start(
                    out=w_planes[32 * quad : 32 * quad + 4 * PASSES, :].bitcast(I32),
                    in_=scale_words[:, 4 * quad : 4 * quad + 4, :],
                )

            w_words = weights.tile([P, PASSES, CHANNELS], U32, align_bytes=64)
            b_all = weights.tile([P, CHANNELS], BF16)
            for gate in GATE_ORDER:
                gate_cols = slice(gate * HIDDEN, (gate + 1) * HIDDEN)
                gate_bytes = slice(gate * HIDDEN * PACK, (gate + 1) * HIDDEN * PACK)
                for g in range(PASSES):
                    nc.sync.dma_start(
                        out=w_words[:, g, gate_cols].bitcast(I32),
                        in_=W_words[g].rearrange("p n t -> p (n t)")[:, gate_bytes].bitcast(I32),
                    )
                nc.sync.dma_start(out=b_all[:, gate_cols], in_=b[gate_cols].partition_broadcast(P))
            for rt in range(SUPER, ROW_TILES):
                nc.sync.dma_start(out=h_raw[:, rt, :], in_=h[rt * P : (rt + 1) * P, :])
            nc.vector.memset(gn_rows[:], 0.0)
            nc.sync.dma_start(
                out=gn_rows[0:gn_pieces, :], in_=gn_weight.rearrange("(t n) -> t n", n=P)
            )
            nc.sync.dma_start(
                out=gn_rows[gn_pieces : 2 * gn_pieces, :],
                in_=gn_bias.rearrange("(t n) -> t n", n=P),
            )
            nc.sync.dma_start(out=c_rows[:], in_=c.rearrange("(r p) n -> p r n", p=P))

            h_codes = weights.tile([P, ROW_TILES, PASSES * P], U32, align_bytes=64)
            h_scales = weights.tile([P, ROW_TILES, PASSES * P], U8, align_bytes=64)
            grouped = {}

            def group_h(rt):
                if not 0 <= rt < ROW_TILES:
                    return
                h_pairs = h_raw[:, rt, :].bitcast(F32)
                h_T = psum.tile([P, BANK], F32, tag="bank")
                pairs_per_pass = K_PASS // 2
                for g in range(PASSES):
                    for u in range(2):
                        block = 2 * g + u
                        nc.tensor.transpose(
                            h_T[:, block * P : (block + 1) * P],
                            h_pairs[:, pairs_per_pass * g + u : pairs_per_pass * (g + 1) : 2],
                            ident[:],
                        )
                grouped[rt] = stage.tile(
                    [P, PASSES * P * PACK], BF16, name="grouped", tag="grouped", align_bytes=64, bufs=SUPER
                )
                nc.scalar.copy(
                    out=grouped[rt][:]
                    .bitcast(F32)
                    .rearrange("p (g r u) -> p g r u", g=PASSES, u=2),
                    in_=h_T[:].rearrange("p (g u r) -> p g r u", g=PASSES, u=2),
                )

            def quantise_h(rt):
                if not 0 <= rt < ROW_TILES:
                    return
                nc.vector.quantize_mx(
                    out=h_codes[:, rt, :].bitcast(FP8X4),
                    scales=h_scales[:, rt, :],
                    in_=grouped[rt][:],
                )

            stats = {}

            def place(unit):
                s, rest = divmod(unit, GATES * SUPER)
                turn, q = divmod(rest, SUPER)
                return GATE_ORDER[turn], s * SUPER + q

            def new_row_tile(unit):
                if not 0 <= unit < UNITS or unit % (GATES * SUPER) >= SUPER:
                    return -1
                return place(unit)[1]

            def last_units(unit):
                return unit >= UNITS - 2

            def statistics_on_vector(unit):
                gate, rt = place(unit)
                group, col = divmod(unit, GROUP)
                parts = small.tile([P, BANKS_PER_GATE, 6], F32)
                for half in range(BANKS_PER_GATE):
                    first = gate * HIDDEN + half * BANK
                    nc.vector.bn_stats(out=parts[:, half, :], in_=x_rows[:, rt, first : first + BANK])
                mean_var = small.tile([P, 2], F32)
                nc.vector.bn_aggr(out=mean_var[:], in_=parts[:].rearrange("p a s -> p (a s)"))
                nc.vector.tensor_scalar(
                    out=stats[("neg_mean", group)][:, col : col + 1],
                    in0=mean_var[:, 0:1],
                    scalar1=-1.0,
                    scalar2=None,
                    op0=ALU.mult,
                )
                nc.vector.tensor_scalar(
                    out=stats[("sum_squares", group)][:, col : col + 1],
                    in0=mean_var[:, 1:2],
                    scalar1=float(HIDDEN),
                    scalar2=None,
                    op0=ALU.mult,
                )

            def add_bias(unit, half):
                if not 0 <= unit < UNITS:
                    return
                gate, rt = place(unit)
                group, col = divmod(unit, GROUP)
                if col == 0 and half == 0:
                    stats[("neg_mean", group)] = small.tile([P, GROUP], F32, name="neg_mean")
                    stats[("sum_squares", group)] = small.tile([P, GROUP], F32, name="sum_squares")
                    stats[("rstd", group)] = small.tile([P, GROUP], F32, name="rstd")
                if half == 0:
                    stats[("sums", unit)] = small.tile([P, BANKS_PER_GATE], F32, name="sums")
                cols = slice(gate * HIDDEN + half * BANK, gate * HIDDEN + (half + 1) * BANK)
                acc = psum.tile([P, BANK], F32, tag="bank")
                for g in range(PASSES):
                    nc.tensor.matmul_mx(
                        out=acc[:],
                        lhsT=h_codes[:, rt, g * P : (g + 1) * P].bitcast(FP8X4),
                        lhsT_scale=h_scales[:, rt, g * P : (g + 1) * P],
                        rhs=w_words[:, g, cols].bitcast(FP8X4),
                        rhs_scale=w_planes[4 * g : P, cols],
                        start=(g == 0),
                        stop=(g == PASSES - 1),
                    )
                nc.vector.scalar_tensor_tensor(
                    out=x_rows[:, rt, cols],
                    in0=b_all[:, cols],
                    scalar=1.0,
                    in1=acc[:],
                    op0=ALU.mult,
                    op1=ALU.add,
                    accum_out=None if last_units(unit) else stats[("sums", unit)][:, half : half + 1],
                )

            def mean_of(unit):
                if not 0 <= unit < UNITS or last_units(unit):
                    return
                group, col = divmod(unit, GROUP)
                sums = stats[("sums", unit)]
                nc.vector.tensor_scalar(
                    out=stats[("neg_mean", group)][:, col : col + 1],
                    in0=sums[:, 0:1],
                    scalar1=sums[:, 1:2],
                    scalar2=-1.0 / HIDDEN,
                    op0=ALU.add,
                    op1=ALU.mult,
                )

            def square(unit):
                if not 0 <= unit < UNITS or last_units(unit):
                    return
                gate, rt = place(unit)
                group, col = divmod(unit, GROUP)
                squares = stage.tile([P, HIDDEN], BF16, bufs=1)
                nc.scalar.activation(
                    out=squares[:],
                    in_=x_rows[:, rt, gate * HIDDEN : (gate + 1) * HIDDEN],
                    func=ACT.Square,
                    bias=stats[("neg_mean", group)][:, col : col + 1],
                    scale=1.0,
                    accum_out=stats[("sum_squares", group)][:, col : col + 1],
                )

            def inverse_std(unit):
                if not 0 <= unit < UNITS or unit % GROUP != GROUP - 1:
                    return
                group = unit // GROUP
                var_eps = small.tile([P, GROUP], F32)
                nc.gpsimd.tensor_scalar(
                    out=var_eps[:],
                    in0=stats[("sum_squares", group)][:],
                    scalar1=1.0 / HIDDEN,
                    scalar2=EPS,
                    op0=ALU.mult,
                    op1=ALU.add,
                )
                nc.gpsimd.tensor_tensor(
                    out=stats[("rstd", group)][:], in0=var_eps[:], in1=minus_half[:], op=ALU.pow
                )

            def normalise(engine, unit):
                gate, rt = place(unit)
                group, col = divmod(unit, GROUP)
                lin = x_rows[:, rt, gate * HIDDEN : (gate + 1) * HIDDEN]
                engine.tensor_scalar(
                    out=lin,
                    in0=lin,
                    scalar1=stats[("neg_mean", group)][:, col : col + 1],
                    scalar2=stats[("rstd", group)][:, col : col + 1],
                    op0=ALU.add,
                    op1=ALU.mult,
                )

            for unit in range(-H_LEAD, UNITS + NORM_LAG):
                ahead = new_row_tile(unit + H_LEAD)
                if ahead >= 0 and ahead % SUPER == 0:
                    for rt in range(ahead, ahead + SUPER):
                        group_h(rt)
                if unit + H_LEAD == UNITS // 2:
                    gn_T = psum.tile([P, P], BF16, tag="bank")
                    nc.tensor.transpose(gn_T[:], gn_rows[:], ident_bf16[:])
                    nc.vector.tensor_copy(out=gn_cols[:], in_=gn_T[:, 0 : 2 * gn_pieces])
                quantise_h(new_row_tile(unit + H_LEAD - 1))
                add_bias(unit, 0)
                mean_of(unit - 1)
                add_bias(unit, 1)
                if unit == UNITS - 1:
                    statistics_on_vector(UNITS - 2)
                    statistics_on_vector(UNITS - 1)
                square(unit - 1)
                inverse_std(unit - 2)
                if 0 <= unit - NORM_LAG < UNITS:
                    normalise(nc.gpsimd, unit - NORM_LAG)

        with ExitStack() as phase:
            work = phase.enter_context(tc.tile_pool(name="work", bufs=4))

            gate_funcs = {
                GATE_I: ACT.Sigmoid, GATE_F: ACT.Sigmoid, GATE_O: ACT.Sigmoid, GATE_G: ACT.Tanh
            }
            tiles = {}

            def flip(name, piece, blocks):
                bank = psum.tile([P, BANK], F32, tag="bank")
                for q in range(SUPER):
                    nc.tensor.transpose(bank[:, q * P : (q + 1) * P], blocks[q], ident[:])
                tiles[(name, piece)] = bank

            def flip_gate(gate, piece):
                if not 0 <= piece < PIECES:
                    return
                s, j = divmod(piece, CH_TILES)
                first = gate * HIDDEN + j * P
                flip(
                    ("x", gate),
                    piece,
                    [x_rows[:, s * SUPER + q, first : first + P] for q in range(SUPER)],
                )

            def activate(gate, piece):
                if not 0 <= piece < PIECES:
                    return
                t = gate * CH_TILES + piece % CH_TILES
                value = work.tile([P, BANK], F32, name="gate%d" % gate)
                nc.scalar.activation(
                    out=value[:],
                    in_=tiles[(("x", gate), piece)][:],
                    func=gate_funcs[gate],
                    scale=gn_cols[:, t : t + 1],
                    bias=gn_cols[:, gn_pieces + t : gn_pieces + t + 1],
                )
                tiles[(gate, piece)] = value

            def input_product(piece):
                if not 0 <= piece < PIECES:
                    return
                i_T = tiles[(GATE_I, piece)]
                nc.vector.tensor_mul(out=i_T[:], in0=i_T[:], in1=tiles[(GATE_G, piece)][:])

            def flip_back(name, gate, piece):
                if not 0 <= piece < PIECES:
                    return
                value = tiles[(gate, piece)]
                flip(name, piece, [value[:, q * P : (q + 1) * P] for q in range(SUPER)])

            def store(value, out, piece):
                s, j = divmod(piece, CH_TILES)
                nc.sync.dma_start(
                    out=out[s * BANK : (s + 1) * BANK, j * P : (j + 1) * P].rearrange(
                        "(q p) n -> p q n", p=P
                    ),
                    in_=value[:],
                )

            def keep_part(piece):
                if not 0 <= piece < PIECES:
                    return
                s, j = divmod(piece, CH_TILES)
                kept = work.tile([P, SUPER, P], F32)
                nc.vector.tensor_mul(
                    out=kept[:],
                    in0=tiles[("f_rows", piece)][:].rearrange("p (q n) -> p q n", q=SUPER),
                    in1=c_rows[:, s * SUPER : (s + 1) * SUPER, j * P : (j + 1) * P],
                )
                tiles[("kept", piece)] = kept

            def new_cell(piece):
                if not 0 <= piece < PIECES:
                    return
                c_new = work.tile([P, SUPER, P], F32)
                nc.vector.tensor_add(
                    out=c_new[:],
                    in0=tiles[("ig_rows", piece)][:].rearrange("p (q n) -> p q n", q=SUPER),
                    in1=tiles[("kept", piece)][:],
                )
                store(c_new, out_1, piece)
                tiles[("c_new", piece)] = c_new

            def tanh_of_cell(piece):
                if not 0 <= piece < PIECES:
                    return
                tanh_c = work.tile([P, SUPER, P], F32)
                nc.scalar.activation(out=tanh_c[:], in_=tiles[("c_new", piece)][:], func=ACT.Tanh)
                tiles[("tanh_c", piece)] = tanh_c

            def hidden(piece):
                if not 0 <= piece < PIECES:
                    return
                h_new = work.tile([P, SUPER, P], F32)
                nc.vector.tensor_mul(
                    out=h_new[:],
                    in0=tiles[("o_rows", piece)][:].rearrange("p (q n) -> p q n", q=SUPER),
                    in1=tiles[("tanh_c", piece)][:],
                )
                store(h_new, out_0, piece)

            for gate in GATE_ORDER:
                flip_gate(gate, 0)
            for piece in range(PIECES + 2):
                flip_back("o_rows", GATE_O, piece - 1)
                hidden(piece - 2)
                new_cell(piece - 1)
                activate(GATE_I, piece)
                flip_gate(GATE_I, piece + 1)
                activate(GATE_G, piece)
                flip_gate(GATE_G, piece + 1)
                input_product(piece)
                activate(GATE_F, piece)
                flip_back("f_rows", GATE_F, piece)
                flip_gate(GATE_F, piece + 1)
                flip_back("ig_rows", GATE_I, piece)
                activate(GATE_O, piece)
                flip_gate(GATE_O, piece + 1)
                tanh_of_cell(piece - 1)
                keep_part(piece)
